import numpy as np
import ml_dtypes


def mxq(x, axis, fmt="e4m3"):
    dtype, down = {"e4m3": (ml_dtypes.float8_e4m3fn, 7), "e5m2": (ml_dtypes.float8_e5m2, 14)}[fmt]
    v = np.moveaxis(np.asarray(x, np.float32).astype(ml_dtypes.bfloat16).astype(np.float64), axis, -1)
    blocks = v.reshape(v.shape[:-1] + (-1, 32))
    amax = np.abs(blocks).max(-1, keepdims=True)
    byte = np.maximum(np.where(amax > 0, np.frexp(amax)[1] - 1 + 127, 0) - down, 1)
    scale = np.exp2(byte - 127.0)
    codes = (blocks / scale).astype(np.float32).astype(dtype).astype(np.float64)
    return np.moveaxis((codes * scale).reshape(v.shape), -1, axis)


WIDE = False


def mx_kscale(k):
    if not WIDE:
        return np.ones(k)
    levels = np.array([10, -10, 5, -5, 0])
    a = np.random.permutation(np.resize(levels, k // 512 * 4)).reshape(k // 512, 4)
    idx = np.arange(k)
    return np.exp2(a[idx // 512, idx % 128 // 32])


BF16 = ml_dtypes.bfloat16


def bf(x):
    return np.asarray(x, np.float32).astype(BF16)


def f64(x):
    return np.asarray(x).astype(np.float64)


B, N, IN_DIM, OUT_DIM, K = 8, 512, 512, 128, 3
EPS = 1e-6
SIG = 2.0


def laplacian(adj):
    d = adj.sum(axis=2)
    r = (d + EPS) ** -0.5
    return np.eye(N)[None] - r[:, :, None] * adj * r[:, None, :]


def setup_inputs():
    s = mx_kscale(N)
    return {"x": bf(np.random.standard_normal((B, N, IN_DIM)) * (s / s.max())[:, None]),
            "adj": bf(np.exp(SIG * np.random.standard_normal((B, N, N)) - SIG * SIG / 2.0) / N * (s * s)[:, None])}


def reference(x, adj):
    L = laplacian(f64(adj))
    return mxq(L, 2, "e4m3") @ mxq(f64(x), 1, "e4m3")

@@ -1,0 +1,146 @@
+from contextlib import ExitStack
+
+import concourse.mybir as mybir
+from concourse.masks import make_identity
+
+F32 = mybir.dt.float32
+BF16 = mybir.dt.bfloat16
+U32 = mybir.dt.uint32
+U8 = mybir.dt.uint8
+FP8X4 = mybir.dt.float8_e4m3fn_x4
+ALU = mybir.AluOpType
+ACT = mybir.ActivationFunctionType
+
+P = 128
+GRAPHS = 8
+NODES = 512
+FEATS = 512
+ROW_TILES = NODES // P
+PACK = 4
+EPS = 1e-6
+
+FLOPS = 2 * GRAPHS * NODES * NODES * FEATS
+
+
+def tile_cheblayer_pa_kernel(tc, x, adj, out):
+    nc = tc.nc
+    with ExitStack() as ctx:
+        const = ctx.enter_context(tc.tile_pool(name="const", bufs=1))
+        loads = ctx.enter_context(tc.tile_pool(name="loads", bufs=GRAPHS))
+        small = ctx.enter_context(tc.tile_pool(name="small", bufs=3))
+        work = ctx.enter_context(tc.tile_pool(name="work", bufs=3))
+        psum_r = ctx.enter_context(tc.psum_pool(name="psum_r", bufs=2))
+        psum_t = ctx.enter_context(tc.psum_pool(name="psum_t", bufs=3))
+        psum_o = ctx.enter_context(tc.psum_pool(name="psum_o", bufs=3))
+
+        eye_f32 = const.tile([P, P], F32)
+        make_identity(nc, eye_f32[:])
+        eye_bf16 = const.tile([P, P], BF16)
+        make_identity(nc, eye_bf16[:])
+        eps = const.tile([P, 1], F32)
+        nc.vector.memset(eps[:], EPS)
+
+        for g in range(GRAPHS):
+            adj_sb = loads.tile([P, ROW_TILES, NODES], BF16)
+            nc.sync.dma_start(out=adj_sb[:], in_=adj[g].rearrange("(m p) j -> p m j", p=P))
+            x_sb = loads.tile([P, PACK, FEATS], BF16)
+            nc.sync.dma_start(out=x_sb[:], in_=x[g].rearrange("(t p) f -> p t f", p=P))
+
+            x_grouped = work.tile([P, FEATS, PACK], BF16, align_bytes=64)
+            nc.vector.tensor_copy(
+                out=x_grouped[:].rearrange("p (c i) t -> p c t i", i=4),
+                in_=x_sb[:].rearrange("p t (c i) -> p c t i", i=4),
+            )
+            x_codes = work.tile([P, FEATS], U32, align_bytes=64)
+            x_scales = work.tile([P, FEATS], U8, align_bytes=64)
+
+            degree = small.tile([P, ROW_TILES], F32)
+            for m in range(ROW_TILES):
+                unread = work.tile([P, NODES], BF16)
+                nc.vector.tensor_scalar(
+                    out=unread[:],
+                    in0=adj_sb[:, m, :],
+                    scalar1=1.0,
+                    scalar2=None,
+                    op0=ALU.mult,
+                    op1=ALU.add,
+                    accum_out=degree[:, m : m + 1],
+                )
+            nc.vector.quantize_mx(
+                out=x_codes[:].bitcast(FP8X4),
+                scales=x_scales[:],
+                in_=x_grouped[:].rearrange("p f t -> p (f t)"),
+            )
+            root = small.tile([P, ROW_TILES], F32)
+            nc.scalar.activation(out=root[:], in_=degree[:], func=ACT.Sqrt, bias=eps[:, 0:1], scale=1.0)
+            r_pos = small.tile([P, ROW_TILES], F32)
+            nc.vector.reciprocal(out=r_pos[:], in_=root[:])
+            r_neg = small.tile([P, ROW_TILES], F32)
+            nc.vector.tensor_scalar_mul(out=r_neg[:], in0=r_pos[:], scalar1=-1.0)
+
+            r_cols = psum_r.tile([P, NODES], F32)
+            for m in range(ROW_TILES):
+                nc.tensor.transpose(
+                    out=r_cols[:, m * P : (m + 1) * P],
+                    in_=r_pos[:, m : m + 1].to_broadcast([P, P]),
+                    identity=eye_f32[:],
+                )
+
+            lap = work.tile([P, ROW_TILES, NODES], BF16)
+            for m in range(ROW_TILES):
+                diag = slice(m * P, (m + 1) * P)
+                scaled = work.tile([P, P], F32)
+                nc.vector.scalar_tensor_tensor(
+                    out=scaled[:],
+                    in0=adj_sb[:, m, diag],
+                    scalar=r_neg[:, m : m + 1],
+                    in1=r_cols[:, diag],
+                    op0=ALU.mult,
+                    op1=ALU.mult,
+                )
+                for lo, hi in ((0, m * P), ((m + 1) * P, NODES)):
+                    if lo < hi:
+                        cols = slice(lo, hi)
+                        nc.vector.scalar_tensor_tensor(
+                            out=lap[:, m, cols],
+                            in0=adj_sb[:, m, cols],
+                            scalar=r_neg[:, m : m + 1],
+                            in1=r_cols[:, cols],
+                            op0=ALU.mult,
+                            op1=ALU.mult,
+                        )
+                nc.vector.tensor_tensor(out=lap[:, m, diag], in0=scaled[:], in1=eye_f32[:], op=ALU.add)
+
+            lap_grouped = work.tile([P, ROW_TILES, P, PACK], BF16, align_bytes=64)
+            for m in range(ROW_TILES):
+                lap_t = psum_t.tile([P, PACK, P], BF16)
+                for t in range(PACK):
+                    nc.tensor.transpose(
+                        out=lap_t[:, t, :],
+                        in_=lap[:, m, t * P : (t + 1) * P],
+                        identity=eye_bf16[:],
+                    )
+                nc.scalar.copy(out=lap_grouped[:, m, :, :], in_=lap_t[:].rearrange("p t c -> p c t"))
+            lap_codes = work.tile([P, NODES], U32, align_bytes=64)
+            lap_scales = work.tile([P, NODES], U8, align_bytes=64)
+            nc.vector.quantize_mx(
+                out=lap_codes[:].bitcast(FP8X4),
+                scales=lap_scales[:],
+                in_=lap_grouped[:].rearrange("p m c t -> p (m c t)"),
+            )
+
+            result = work.tile([P, ROW_TILES, FEATS], F32)
+            for m in range(ROW_TILES):
+                rows = slice(m * P, (m + 1) * P)
+                acc = psum_o.tile([P, FEATS], F32)
+                nc.tensor.matmul_mx(
+                    out=acc[:],
+                    lhsT=lap_codes[:, rows].bitcast(FP8X4),
+                    lhsT_scale=lap_scales[:, rows],
+                    rhs=x_codes[:].bitcast(FP8X4),
+                    rhs_scale=x_scales[:],
+                    start=True,
+                    stop=True,
+                )
+                nc.scalar.copy(out=result[:, m, :], in_=acc[:])
+            nc.sync.dma_start(out=out[g].rearrange("(m p) f -> p m f", p=P), in_=result[:])

@@ -16,8 +16,11 @@ GRAPHS = 8
 NODES = 512
 FEATS = 512
 ROW_TILES = NODES // P
+UNITS = GRAPHS * ROW_TILES
 PACK = 4
 EPS = 1e-6
+GROUP = 2
+LAG = 2
 
 FLOPS = 2 * GRAPHS * NODES * NODES * FEATS
 
@@ -25,10 +28,11 @@ FLOPS = 2 * GRAPHS * NODES * NODES * FEATS
 def tile_cheblayer_pa_kernel(tc, x, adj, out):
     nc = tc.nc
     with ExitStack() as ctx:
+        ctx.enter_context(tc.manual_schedule())
         const = ctx.enter_context(tc.tile_pool(name="const", bufs=1))
         loads = ctx.enter_context(tc.tile_pool(name="loads", bufs=GRAPHS))
-        small = ctx.enter_context(tc.tile_pool(name="small", bufs=3))
-        work = ctx.enter_context(tc.tile_pool(name="work", bufs=3))
+        per_graph = ctx.enter_context(tc.tile_pool(name="per_graph", bufs=3))
+        per_unit = ctx.enter_context(tc.tile_pool(name="per_unit", bufs=LAG + GROUP + 2))
         psum_r = ctx.enter_context(tc.psum_pool(name="psum_r", bufs=2))
         psum_t = ctx.enter_context(tc.psum_pool(name="psum_t", bufs=3))
         psum_o = ctx.enter_context(tc.psum_pool(name="psum_o", bufs=3))
@@ -40,44 +44,43 @@ def tile_cheblayer_pa_kernel(tc, x, adj, out):
         eps = const.tile([P, 1], F32)
         nc.vector.memset(eps[:], EPS)
 
-        for g in range(GRAPHS):
+        adj_of, x_of, degree_of, root_of, r_neg_of, r_cols_of = {}, {}, {}, {}, {}, {}
+        x_grouped_of, x_codes_of, x_scales_of, lap_grouped_of = {}, {}, {}, {}
+
+        def load_adj(g):
             adj_sb = loads.tile([P, ROW_TILES, NODES], BF16)
             nc.sync.dma_start(out=adj_sb[:], in_=adj[g].rearrange("(m p) j -> p m j", p=P))
+            adj_of[g] = adj_sb
+
+        def load_x(g):
             x_sb = loads.tile([P, PACK, FEATS], BF16)
             nc.sync.dma_start(out=x_sb[:], in_=x[g].rearrange("(t p) f -> p t f", p=P))
+            x_of[g] = x_sb
 
-            x_grouped = work.tile([P, FEATS, PACK], BF16, align_bytes=64)
-            nc.vector.tensor_copy(
-                out=x_grouped[:].rearrange("p (c i) t -> p c t i", i=4),
-                in_=x_sb[:].rearrange("p t (c i) -> p c t i", i=4),
+        def row_sum(g, m):
+            if m == 0:
+                degree = per_graph.tile([P, ROW_TILES], F32)
+                degree_of[g] = degree
+            unread = per_unit.tile([P, NODES], BF16)
+            nc.vector.tensor_scalar(
+                out=unread[:],
+                in0=adj_of[g][:, m, :],
+                scalar1=1.0,
+                scalar2=None,
+                op0=ALU.mult,
+                op1=ALU.add,
+                accum_out=degree_of[g][:, m : m + 1],
             )
-            x_codes = work.tile([P, FEATS], U32, align_bytes=64)
-            x_scales = work.tile([P, FEATS], U8, align_bytes=64)
+            if m == ROW_TILES - 1:
+                root = per_graph.tile([P, ROW_TILES], F32)
+                nc.scalar.activation(out=root[:], in_=degree_of[g][:], func=ACT.Sqrt, bias=eps[:, 0:1], scale=1.0)
+                root_of[g] = root
 
-            degree = small.tile([P, ROW_TILES], F32)
-            for m in range(ROW_TILES):
-                unread = work.tile([P, NODES], BF16)
-                nc.vector.tensor_scalar(
-                    out=unread[:],
-                    in0=adj_sb[:, m, :],
-                    scalar1=1.0,
-                    scalar2=None,
-                    op0=ALU.mult,
-                    op1=ALU.add,
-                    accum_out=degree[:, m : m + 1],
-                )
-            nc.vector.quantize_mx(
-                out=x_codes[:].bitcast(FP8X4),
-                scales=x_scales[:],
-                in_=x_grouped[:].rearrange("p f t -> p (f t)"),
-            )
-            root = small.tile([P, ROW_TILES], F32)
-            nc.scalar.activation(out=root[:], in_=degree[:], func=ACT.Sqrt, bias=eps[:, 0:1], scale=1.0)
-            r_pos = small.tile([P, ROW_TILES], F32)
-            nc.vector.reciprocal(out=r_pos[:], in_=root[:])
-            r_neg = small.tile([P, ROW_TILES], F32)
+        def inverse_roots(g):
+            r_pos = per_graph.tile([P, ROW_TILES], F32)
+            nc.vector.reciprocal(out=r_pos[:], in_=root_of[g][:])
+            r_neg = per_graph.tile([P, ROW_TILES], F32)
             nc.vector.tensor_scalar_mul(out=r_neg[:], in0=r_pos[:], scalar1=-1.0)
-
             r_cols = psum_r.tile([P, NODES], F32)
             for m in range(ROW_TILES):
                 nc.tensor.transpose(
@@ -85,62 +88,109 @@ def tile_cheblayer_pa_kernel(tc, x, adj, out):
                     in_=r_pos[:, m : m + 1].to_broadcast([P, P]),
                     identity=eye_f32[:],
                 )
+            r_neg_of[g] = r_neg
+            r_cols_of[g] = r_cols
 
-            lap = work.tile([P, ROW_TILES, NODES], BF16)
-            for m in range(ROW_TILES):
-                diag = slice(m * P, (m + 1) * P)
-                scaled = work.tile([P, P], F32)
-                nc.vector.scalar_tensor_tensor(
-                    out=scaled[:],
-                    in0=adj_sb[:, m, diag],
-                    scalar=r_neg[:, m : m + 1],
-                    in1=r_cols[:, diag],
-                    op0=ALU.mult,
-                    op1=ALU.mult,
-                )
-                for lo, hi in ((0, m * P), ((m + 1) * P, NODES)):
-                    if lo < hi:
-                        cols = slice(lo, hi)
-                        nc.vector.scalar_tensor_tensor(
-                            out=lap[:, m, cols],
-                            in0=adj_sb[:, m, cols],
-                            scalar=r_neg[:, m : m + 1],
-                            in1=r_cols[:, cols],
-                            op0=ALU.mult,
-                            op1=ALU.mult,
-                        )
-                nc.vector.tensor_tensor(out=lap[:, m, diag], in0=scaled[:], in1=eye_f32[:], op=ALU.add)
+        def regroup_x(g, quarter):
+            if quarter == 0:
+                x_grouped = per_graph.tile([P, FEATS, PACK], BF16, align_bytes=64)
+                x_grouped_of[g] = x_grouped
+            cols = slice(quarter * P, (quarter + 1) * P)
+            nc.gpsimd.tensor_scalar(
+                out=x_grouped_of[g][:, cols, :],
+                in0=x_of[g][:, :, cols].rearrange("p t f -> p f t"),
+                scalar1=1.0,
+                scalar2=0.0,
+                op0=ALU.mult,
+                op1=ALU.add,
+            )
 
-            lap_grouped = work.tile([P, ROW_TILES, P, PACK], BF16, align_bytes=64)
-            for m in range(ROW_TILES):
-                lap_t = psum_t.tile([P, PACK, P], BF16)
-                for t in range(PACK):
-                    nc.tensor.transpose(
-                        out=lap_t[:, t, :],
-                        in_=lap[:, m, t * P : (t + 1) * P],
-                        identity=eye_bf16[:],
-                    )
-                nc.scalar.copy(out=lap_grouped[:, m, :, :], in_=lap_t[:].rearrange("p t c -> p c t"))
-            lap_codes = work.tile([P, NODES], U32, align_bytes=64)
-            lap_scales = work.tile([P, NODES], U8, align_bytes=64)
+        def quantise_x(g):
+            x_codes = per_graph.tile([P, FEATS], U32, align_bytes=64)
+            x_scales = per_graph.tile([P, FEATS], U8, align_bytes=64)
+            nc.vector.quantize_mx(
+                out=x_codes[:].bitcast(FP8X4),
+                scales=x_scales[:],
+                in_=x_grouped_of[g][:].rearrange("p f t -> p (f t)"),
+            )
+            x_codes_of[g] = x_codes
+            x_scales_of[g] = x_scales
+
+        def scale_columns(g, m, cols, dest):
+            nc.vector.scalar_tensor_tensor(
+                out=dest,
+                in0=adj_of[g][:, m, cols],
+                scalar=r_neg_of[g][:, m : m + 1],
+                in1=r_cols_of[g][:, cols],
+                op0=ALU.mult,
+                op1=ALU.mult,
+            )
+
+        def laplacian(g, m):
+            diag = slice(m * P, (m + 1) * P)
+            lap = per_unit.tile([P, NODES], BF16)
+            scaled = per_unit.tile([P, P], F32)
+            scale_columns(g, m, diag, scaled[:])
+            nc.gpsimd.tensor_tensor(out=lap[:, diag], in0=scaled[:], in1=eye_f32[:], op=ALU.add)
+            if m > 0:
+                scale_columns(g, m, slice(0, m * P), lap[:, 0 : m * P])
+            if m < ROW_TILES - 1:
+                scale_columns(g, m, slice((m + 1) * P, NODES), lap[:, (m + 1) * P : NODES])
+            lap_t = psum_t.tile([P, PACK, P], BF16)
+            for t in range(PACK):
+                nc.tensor.transpose(out=lap_t[:, t, :], in_=lap[:, t * P : (t + 1) * P], identity=eye_bf16[:])
+            lap_grouped = per_unit.tile([P, P, PACK], BF16, align_bytes=64)
+            nc.scalar.copy(out=lap_grouped[:], in_=lap_t[:].rearrange("p t c -> p c t"))
+            lap_grouped_of[(g, m)] = lap_grouped
+
+        def multiply(g, m):
+            lap_codes = per_unit.tile([P, P], U32, align_bytes=64)
+            lap_scales = per_unit.tile([P, P], U8, align_bytes=64)
             nc.vector.quantize_mx(
                 out=lap_codes[:].bitcast(FP8X4),
                 scales=lap_scales[:],
-                in_=lap_grouped[:].rearrange("p m c t -> p (m c t)"),
+                in_=lap_grouped_of[(g, m)][:].rearrange("p c t -> p (c t)"),
             )
+            acc = psum_o.tile([P, FEATS], F32)
+            nc.tensor.matmul_mx(
+                out=acc[:],
+                lhsT=lap_codes[:].bitcast(FP8X4),
+                lhsT_scale=lap_scales[:],
+                rhs=x_codes_of[g][:].bitcast(FP8X4),
+                rhs_scale=x_scales_of[g][:],
+                start=True,
+                stop=True,
+            )
+            result = per_unit.tile([P, FEATS], F32)
+            nc.scalar.copy(out=result[:], in_=acc[:])
+            nc.sync.dma_start(out=out[g, m * P : (m + 1) * P, :], in_=result[:])
 
-            result = work.tile([P, ROW_TILES, FEATS], F32)
+        load_adj(0)
+        load_adj(1)
+        for g in range(GRAPHS):
+            load_x(g)
+            if g + 2 < GRAPHS:
+                load_adj(g + 2)
+
+        for g in range(2):
             for m in range(ROW_TILES):
-                rows = slice(m * P, (m + 1) * P)
-                acc = psum_o.tile([P, FEATS], F32)
-                nc.tensor.matmul_mx(
-                    out=acc[:],
-                    lhsT=lap_codes[:, rows].bitcast(FP8X4),
-                    lhsT_scale=lap_scales[:, rows],
-                    rhs=x_codes[:].bitcast(FP8X4),
-                    rhs_scale=x_scales[:],
-                    start=True,
-                    stop=True,
-                )
-                nc.scalar.copy(out=result[:, m, :], in_=acc[:])
-            nc.sync.dma_start(out=out[g].rearrange("(m p) f -> p m f", p=P), in_=result[:])
+                row_sum(g, m)
+        inverse_roots(0)
+        for quarter in range(ROW_TILES):
+            regroup_x(0, quarter)
+
+        for first in range(0, UNITS + LAG, GROUP):
+            for u in range(first, min(first + GROUP, UNITS)):
+                g, m = divmod(u, ROW_TILES)
+                laplacian(g, m)
+                if g + 2 < GRAPHS:
+                    row_sum(g + 2, m)
+                if g + 1 < GRAPHS:
+                    regroup_x(g + 1, m)
+                if m == 1:
+                    quantise_x(g)
+                if m == 2 and g + 1 < GRAPHS:
+                    inverse_roots(g + 1)
+            for u in range(max(first - LAG, 0), first - LAG + GROUP):
+                g, m = divmod(u, ROW_TILES)
+                multiply(g, m)

@@ -35,7 +35,8 @@ def tile_cheblayer_pa_kernel(tc, x, adj, out):
         per_unit = ctx.enter_context(tc.tile_pool(name="per_unit", bufs=LAG + GROUP + 2))
         psum_r = ctx.enter_context(tc.psum_pool(name="psum_r", bufs=2))
         psum_t = ctx.enter_context(tc.psum_pool(name="psum_t", bufs=3))
-        psum_o = ctx.enter_context(tc.psum_pool(name="psum_o", bufs=3))
+        psum_o = ctx.enter_context(tc.psum_pool(name="psum_o", bufs=GROUP))
+        psum_c = ctx.enter_context(tc.psum_pool(name="psum_c", bufs=1))
 
         eye_f32 = const.tile([P, P], F32)
         make_identity(nc, eye_f32[:])
@@ -43,6 +44,8 @@ def tile_cheblayer_pa_kernel(tc, x, adj, out):
         make_identity(nc, eye_bf16[:])
         eps = const.tile([P, 1], F32)
         nc.vector.memset(eps[:], EPS)
+        eye_psum = psum_c.tile([P, P], F32)
+        nc.tensor.transpose(out=eye_psum[:], in_=eye_f32[:], identity=eye_f32[:])
 
         adj_of, x_of, degree_of, root_of, r_neg_of, r_cols_of = {}, {}, {}, {}, {}, {}
         x_grouped_of, x_codes_of, x_scales_of, lap_grouped_of = {}, {}, {}, {}
@@ -59,26 +62,39 @@ def tile_cheblayer_pa_kernel(tc, x, adj, out):
 
         def row_sum(g, m):
             if m == 0:
-                degree = per_graph.tile([P, ROW_TILES], F32)
-                degree_of[g] = degree
-            unread = per_unit.tile([P, NODES], BF16)
-            nc.vector.tensor_scalar(
-                out=unread[:],
-                in0=adj_of[g][:, m, :],
-                scalar1=1.0,
-                scalar2=None,
-                op0=ALU.mult,
-                op1=ALU.add,
-                accum_out=degree_of[g][:, m : m + 1],
-            )
+                degree_even = per_graph.tile([P, ROW_TILES // 2], F32)
+                degree_odd = per_graph.tile([P, ROW_TILES // 2], F32)
+                degree_of[g] = (degree_even, degree_odd)
+            total = degree_of[g][m % 2][:, m // 2 : m // 2 + 1]
+            if m % 2 == 0:
+                unread_v = per_unit.tile([P, NODES], BF16)
+                nc.vector.tensor_scalar(
+                    out=unread_v[:],
+                    in0=adj_of[g][:, m, :],
+                    scalar1=1.0,
+                    scalar2=None,
+                    op0=ALU.mult,
+                    op1=ALU.add,
+                    accum_out=total,
+                )
+            else:
+                unread_s = per_unit.tile([P, NODES], BF16)
+                nc.scalar.activation(out=unread_s[:], in_=adj_of[g][:, m, :], func=ACT.Copy, accum_out=total)
             if m == ROW_TILES - 1:
-                root = per_graph.tile([P, ROW_TILES], F32)
-                nc.scalar.activation(out=root[:], in_=degree_of[g][:], func=ACT.Sqrt, bias=eps[:, 0:1], scale=1.0)
+                root = per_graph.tile([P, ROW_TILES // 2, 2], F32)
+                for parity in range(2):
+                    nc.scalar.activation(
+                        out=root[:, :, parity],
+                        in_=degree_of[g][parity][:],
+                        func=ACT.Sqrt,
+                        bias=eps[:, 0:1],
+                        scale=1.0,
+                    )
                 root_of[g] = root
 
         def inverse_roots(g):
             r_pos = per_graph.tile([P, ROW_TILES], F32)
-            nc.vector.reciprocal(out=r_pos[:], in_=root_of[g][:])
+            nc.vector.reciprocal(out=r_pos[:], in_=root_of[g][:].rearrange("p k two -> p (k two)"))
             r_neg = per_graph.tile([P, ROW_TILES], F32)
             nc.vector.tensor_scalar_mul(out=r_neg[:], in0=r_pos[:], scalar1=-1.0)
             r_cols = psum_r.tile([P, NODES], F32)
@@ -131,11 +147,11 @@ def tile_cheblayer_pa_kernel(tc, x, adj, out):
             lap = per_unit.tile([P, NODES], BF16)
             scaled = per_unit.tile([P, P], F32)
             scale_columns(g, m, diag, scaled[:])
-            nc.gpsimd.tensor_tensor(out=lap[:, diag], in0=scaled[:], in1=eye_f32[:], op=ALU.add)
             if m > 0:
                 scale_columns(g, m, slice(0, m * P), lap[:, 0 : m * P])
             if m < ROW_TILES - 1:
                 scale_columns(g, m, slice((m + 1) * P, NODES), lap[:, (m + 1) * P : NODES])
+            nc.vector.tensor_tensor(out=lap[:, diag], in0=scaled[:], in1=eye_psum[:], op=ALU.add)
             lap_t = psum_t.tile([P, PACK, P], BF16)
             for t in range(PACK):
                 nc.tensor.transpose(out=lap_t[:, t, :], in_=lap[:, t * P : (t + 1) * P], identity=eye_bf16[:])
@@ -182,9 +198,9 @@ def tile_cheblayer_pa_kernel(tc, x, adj, out):
         for first in range(0, UNITS + LAG, GROUP):
             for u in range(first, min(first + GROUP, UNITS)):
                 g, m = divmod(u, ROW_TILES)
-                laplacian(g, m)
                 if g + 2 < GRAPHS:
                     row_sum(g + 2, m)
+                laplacian(g, m)
                 if g + 1 < GRAPHS:
                     regroup_x(g + 1, m)
                 if m == 1:

@@ -18,6 +18,9 @@ FEATS = 512
 ROW_TILES = NODES // P
 UNITS = GRAPHS * ROW_TILES
 PACK = 4
+HALVES = 2
+PAIR = 2
+OWN_BLOCK = 8
 EPS = 1e-6
 GROUP = 2
 LAG = 2
@@ -40,15 +43,15 @@ def tile_cheblayer_pa_kernel(tc, x, adj, out):
 
         eye_f32 = const.tile([P, P], F32)
         make_identity(nc, eye_f32[:])
-        eye_bf16 = const.tile([P, P], BF16)
-        make_identity(nc, eye_bf16[:])
         eps = const.tile([P, 1], F32)
         nc.vector.memset(eps[:], EPS)
+        table_warmer = const.tile([P, 1], F32)
+        nc.scalar.activation(out=table_warmer[:], in_=eps[:], func=ACT.Sqrt)
         eye_psum = psum_c.tile([P, P], F32)
         nc.tensor.transpose(out=eye_psum[:], in_=eye_f32[:], identity=eye_f32[:])
 
         adj_of, x_of, degree_of, root_of, r_neg_of, r_cols_of = {}, {}, {}, {}, {}, {}
-        x_grouped_of, x_codes_of, x_scales_of, lap_grouped_of = {}, {}, {}, {}
+        x_grouped_of, x_codes_of, x_scales_of, lap_of, lap_grouped_of = {}, {}, {}, {}, {}
 
         def load_adj(g):
             adj_sb = loads.tile([P, ROW_TILES, NODES], BF16)
@@ -57,16 +60,18 @@ def tile_cheblayer_pa_kernel(tc, x, adj, out):
 
         def load_x(g):
             x_sb = loads.tile([P, PACK, FEATS], BF16)
-            nc.sync.dma_start(out=x_sb[:], in_=x[g].rearrange("(t p) f -> p t f", p=P))
+            nc.sync.dma_start(
+                out=x_sb[:].rearrange("p (u e) f -> p u e f", u=HALVES),
+                in_=x[g].rearrange("(u p e) f -> p u e f", u=HALVES, e=PAIR),
+            )
             x_of[g] = x_sb
 
         def row_sum(g, m):
             if m == 0:
-                degree_even = per_graph.tile([P, ROW_TILES // 2], F32)
-                degree_odd = per_graph.tile([P, ROW_TILES // 2], F32)
-                degree_of[g] = (degree_even, degree_odd)
-            total = degree_of[g][m % 2][:, m // 2 : m // 2 + 1]
-            if m % 2 == 0:
+                degree = per_graph.tile([P, ROW_TILES, OWN_BLOCK], F32)
+                degree_of[g] = degree
+            total = degree_of[g][:, m, 0:1]
+            if m == 0 or g == 0:
                 unread_v = per_unit.tile([P, NODES], BF16)
                 nc.vector.tensor_scalar(
                     out=unread_v[:],
@@ -81,20 +86,15 @@ def tile_cheblayer_pa_kernel(tc, x, adj, out):
                 unread_s = per_unit.tile([P, NODES], BF16)
                 nc.scalar.activation(out=unread_s[:], in_=adj_of[g][:, m, :], func=ACT.Copy, accum_out=total)
             if m == ROW_TILES - 1:
-                root = per_graph.tile([P, ROW_TILES // 2, 2], F32)
-                for parity in range(2):
-                    nc.scalar.activation(
-                        out=root[:, :, parity],
-                        in_=degree_of[g][parity][:],
-                        func=ACT.Sqrt,
-                        bias=eps[:, 0:1],
-                        scale=1.0,
-                    )
+                root = per_graph.tile([P, ROW_TILES], F32)
+                nc.scalar.activation(
+                    out=root[:], in_=degree_of[g][:, :, 0], func=ACT.Sqrt, bias=eps[:, 0:1], scale=1.0
+                )
                 root_of[g] = root
 
         def inverse_roots(g):
             r_pos = per_graph.tile([P, ROW_TILES], F32)
-            nc.vector.reciprocal(out=r_pos[:], in_=root_of[g][:].rearrange("p k two -> p (k two)"))
+            nc.vector.reciprocal(out=r_pos[:], in_=root_of[g][:])
             r_neg = per_graph.tile([P, ROW_TILES], F32)
             nc.vector.tensor_scalar_mul(out=r_neg[:], in0=r_pos[:], scalar1=-1.0)
             r_cols = psum_r.tile([P, NODES], F32)
@@ -152,11 +152,18 @@ def tile_cheblayer_pa_kernel(tc, x, adj, out):
             if m < ROW_TILES - 1:
                 scale_columns(g, m, slice((m + 1) * P, NODES), lap[:, (m + 1) * P : NODES])
             nc.vector.tensor_tensor(out=lap[:, diag], in0=scaled[:], in1=eye_psum[:], op=ALU.add)
-            lap_t = psum_t.tile([P, PACK, P], BF16)
-            for t in range(PACK):
-                nc.tensor.transpose(out=lap_t[:, t, :], in_=lap[:, t * P : (t + 1) * P], identity=eye_bf16[:])
-            lap_grouped = per_unit.tile([P, P, PACK], BF16, align_bytes=64)
-            nc.scalar.copy(out=lap_grouped[:], in_=lap_t[:].rearrange("p t c -> p c t"))
+            lap_of[(g, m)] = lap
+
+        def transpose_laplacian(g, m):
+            lap_words = lap_of[(g, m)][:].bitcast(F32)
+            lap_t = psum_t.tile([P, HALVES, P], F32)
+            for u in range(HALVES):
+                nc.tensor.transpose(out=lap_t[:, u, :], in_=lap_words[:, u * P : (u + 1) * P], identity=eye_f32[:])
+            lap_grouped = per_unit.tile([P, P * PACK], BF16, align_bytes=64)
+            nc.scalar.copy(
+                out=lap_grouped[:].bitcast(F32).rearrange("p (c u) -> p c u", u=HALVES),
+                in_=lap_t[:].rearrange("p u c -> p c u"),
+            )
             lap_grouped_of[(g, m)] = lap_grouped
 
         def multiply(g, m):
@@ -165,7 +172,7 @@ def tile_cheblayer_pa_kernel(tc, x, adj, out):
             nc.vector.quantize_mx(
                 out=lap_codes[:].bitcast(FP8X4),
                 scales=lap_scales[:],
-                in_=lap_grouped_of[(g, m)][:].rearrange("p c t -> p (c t)"),
+                in_=lap_grouped_of[(g, m)][:],
             )
             acc = psum_o.tile([P, FEATS], F32)
             nc.tensor.matmul_mx(
@@ -196,17 +203,18 @@ def tile_cheblayer_pa_kernel(tc, x, adj, out):
             regroup_x(0, quarter)
 
         for first in range(0, UNITS + LAG, GROUP):
-            for u in range(first, min(first + GROUP, UNITS)):
-                g, m = divmod(u, ROW_TILES)
+            for unit in range(first, min(first + GROUP, UNITS)):
+                g, m = divmod(unit, ROW_TILES)
+                laplacian(g, m)
                 if g + 2 < GRAPHS:
                     row_sum(g + 2, m)
-                laplacian(g, m)
+                transpose_laplacian(g, m)
                 if g + 1 < GRAPHS:
                     regroup_x(g + 1, m)
                 if m == 1:
                     quantise_x(g)
                 if m == 2 and g + 1 < GRAPHS:
                     inverse_roots(g + 1)
-            for u in range(max(first - LAG, 0), first - LAG + GROUP):
-                g, m = divmod(u, ROW_TILES)
+            for unit in range(max(first - LAG, 0), first - LAG + GROUP):
+                g, m = divmod(unit, ROW_TILES)
                 multiply(g, m)

@@ -36,6 +36,7 @@ def tile_cheblayer_pa_kernel(tc, x, adj, out):
         loads = ctx.enter_context(tc.tile_pool(name="loads", bufs=GRAPHS))
         per_graph = ctx.enter_context(tc.tile_pool(name="per_graph", bufs=3))
         per_unit = ctx.enter_context(tc.tile_pool(name="per_unit", bufs=LAG + GROUP + 2))
+        results = ctx.enter_context(tc.tile_pool(name="results", bufs=UNITS))
         psum_r = ctx.enter_context(tc.psum_pool(name="psum_r", bufs=2))
         psum_t = ctx.enter_context(tc.psum_pool(name="psum_t", bufs=3))
         psum_o = ctx.enter_context(tc.psum_pool(name="psum_o", bufs=GROUP))
@@ -184,7 +185,7 @@ def tile_cheblayer_pa_kernel(tc, x, adj, out):
                 start=True,
                 stop=True,
             )
-            result = per_unit.tile([P, FEATS], F32)
+            result = results.tile([P, FEATS], F32)
             nc.scalar.copy(out=result[:], in_=acc[:])
             nc.sync.dma_start(out=out[g, m * P : (m + 1) * P, :], in_=result[:])
 

@@ -24,6 +24,7 @@ OWN_BLOCK = 8
 EPS = 1e-6
 GROUP = 2
 LAG = 2
+VECTOR_SUMS = 2
 
 FLOPS = 2 * GRAPHS * NODES * NODES * FEATS
 
@@ -72,7 +73,7 @@ def tile_cheblayer_pa_kernel(tc, x, adj, out):
                 degree = per_graph.tile([P, ROW_TILES, OWN_BLOCK], F32)
                 degree_of[g] = degree
             total = degree_of[g][:, m, 0:1]
-            if m == 0 or g == 0:
+            if m < VECTOR_SUMS or g == 0:
                 unread_v = per_unit.tile([P, NODES], BF16)
                 nc.vector.tensor_scalar(
                     out=unread_v[:],

@@ -23,8 +23,9 @@ PAIR = 2
 OWN_BLOCK = 8
 EPS = 1e-6
 GROUP = 2
-LAG = 2
-VECTOR_SUMS = 2
+PITCH = NODES + P
+LAP_WIDTH = (ROW_TILES - GROUP) * P + GROUP * PITCH
+SCALAR_ALONE = 2
 
 FLOPS = 2 * GRAPHS * NODES * NODES * FEATS
 
@@ -36,10 +37,11 @@ def tile_cheblayer_pa_kernel(tc, x, adj, out):
         const = ctx.enter_context(tc.tile_pool(name="const", bufs=1))
         loads = ctx.enter_context(tc.tile_pool(name="loads", bufs=GRAPHS))
         per_graph = ctx.enter_context(tc.tile_pool(name="per_graph", bufs=3))
-        per_unit = ctx.enter_context(tc.tile_pool(name="per_unit", bufs=LAG + GROUP + 2))
+        per_unit = ctx.enter_context(tc.tile_pool(name="per_unit", bufs=4))
+        per_pair = ctx.enter_context(tc.tile_pool(name="per_pair", bufs=3))
         results = ctx.enter_context(tc.tile_pool(name="results", bufs=UNITS))
         psum_r = ctx.enter_context(tc.psum_pool(name="psum_r", bufs=2))
-        psum_t = ctx.enter_context(tc.psum_pool(name="psum_t", bufs=3))
+        psum_t = ctx.enter_context(tc.psum_pool(name="psum_t", bufs=2))
         psum_o = ctx.enter_context(tc.psum_pool(name="psum_o", bufs=GROUP))
         psum_c = ctx.enter_context(tc.psum_pool(name="psum_c", bufs=1))
 
@@ -49,8 +51,9 @@ def tile_cheblayer_pa_kernel(tc, x, adj, out):
         nc.vector.memset(eps[:], EPS)
         table_warmer = const.tile([P, 1], F32)
         nc.scalar.activation(out=table_warmer[:], in_=eps[:], func=ACT.Sqrt)
-        eye_psum = psum_c.tile([P, P], F32)
-        nc.tensor.transpose(out=eye_psum[:], in_=eye_f32[:], identity=eye_f32[:])
+        eye_pair = psum_c.tile([P, GROUP, P], F32)
+        for local in range(GROUP):
+            nc.tensor.transpose(out=eye_pair[:, local, :], in_=eye_f32[:], identity=eye_f32[:])
 
         adj_of, x_of, degree_of, root_of, r_neg_of, r_cols_of = {}, {}, {}, {}, {}, {}
         x_grouped_of, x_codes_of, x_scales_of, lap_of, lap_grouped_of = {}, {}, {}, {}, {}
@@ -73,7 +76,13 @@ def tile_cheblayer_pa_kernel(tc, x, adj, out):
                 degree = per_graph.tile([P, ROW_TILES, OWN_BLOCK], F32)
                 degree_of[g] = degree
             total = degree_of[g][:, m, 0:1]
-            if m < VECTOR_SUMS or g == 0:
+            if g == 0:
+                on_vector = m < ROW_TILES - 1
+            elif g <= SCALAR_ALONE:
+                on_vector = False
+            else:
+                on_vector = m % GROUP == 0
+            if on_vector:
                 unread_v = per_unit.tile([P, NODES], BF16)
                 nc.vector.tensor_scalar(
                     out=unread_v[:],
@@ -144,51 +153,71 @@ def tile_cheblayer_pa_kernel(tc, x, adj, out):
                 op1=ALU.mult,
             )
 
-        def laplacian(g, m):
-            diag = slice(m * P, (m + 1) * P)
-            lap = per_unit.tile([P, NODES], BF16)
-            scaled = per_unit.tile([P, P], F32)
-            scale_columns(g, m, diag, scaled[:])
-            if m > 0:
-                scale_columns(g, m, slice(0, m * P), lap[:, 0 : m * P])
-            if m < ROW_TILES - 1:
-                scale_columns(g, m, slice((m + 1) * P, NODES), lap[:, (m + 1) * P : NODES])
-            nc.vector.tensor_tensor(out=lap[:, diag], in0=scaled[:], in1=eye_psum[:], op=ALU.add)
-            lap_of[(g, m)] = lap
+        def laplacian(g, first_m):
+            lap_pair = per_pair.tile([P, LAP_WIDTH], BF16)
+            scaled = per_pair.tile([P, GROUP, P], F32)
+            for local in range(GROUP):
+                m = first_m + local
+                scale_columns(g, m, slice(m * P, (m + 1) * P), scaled[:, local, :])
+            for local in range(GROUP):
+                m = first_m + local
+                lap = lap_pair[:, local * NODES : (local + 1) * NODES]
+                if m > 0:
+                    scale_columns(g, m, slice(0, m * P), lap[:, 0 : m * P])
+                if m < ROW_TILES - 1:
+                    scale_columns(g, m, slice((m + 1) * P, NODES), lap[:, (m + 1) * P : NODES])
+            nc.vector.tensor_tensor(
+                out=lap_pair[:, first_m * P : first_m * P + GROUP * PITCH].rearrange("p (l w) -> p l w", w=PITCH)[
+                    :, :, 0:P
+                ],
+                in0=scaled[:],
+                in1=eye_pair[:],
+                op=ALU.add,
+            )
+            lap_of[(g, first_m)] = lap_pair
 
-        def transpose_laplacian(g, m):
-            lap_words = lap_of[(g, m)][:].bitcast(F32)
-            lap_t = psum_t.tile([P, HALVES, P], F32)
-            for u in range(HALVES):
-                nc.tensor.transpose(out=lap_t[:, u, :], in_=lap_words[:, u * P : (u + 1) * P], identity=eye_f32[:])
-            lap_grouped = per_unit.tile([P, P * PACK], BF16, align_bytes=64)
+        def transpose_laplacian(g, first_m):
+            lap_words = lap_of[(g, first_m)][:, 0 : GROUP * NODES].bitcast(F32)
+            words = NODES // PAIR
+            lap_t = psum_t.tile([P, HALVES, GROUP * P], F32)
+            for local in range(GROUP):
+                for u in range(HALVES):
+                    nc.tensor.transpose(
+                        out=lap_t[:, u, local * P : (local + 1) * P],
+                        in_=lap_words[:, local * words + u * P : local * words + (u + 1) * P],
+                        identity=eye_f32[:],
+                    )
+            lap_grouped = per_pair.tile([P, GROUP * P * PACK], BF16, align_bytes=64)
             nc.scalar.copy(
                 out=lap_grouped[:].bitcast(F32).rearrange("p (c u) -> p c u", u=HALVES),
                 in_=lap_t[:].rearrange("p u c -> p c u"),
             )
-            lap_grouped_of[(g, m)] = lap_grouped
+            lap_grouped_of[(g, first_m)] = lap_grouped
 
-        def multiply(g, m):
-            lap_codes = per_unit.tile([P, P], U32, align_bytes=64)
-            lap_scales = per_unit.tile([P, P], U8, align_bytes=64)
+        def multiply(g, first_m):
+            lap_codes = per_pair.tile([P, GROUP * P], U32, align_bytes=64)
+            lap_scales = per_pair.tile([P, GROUP * P], U8, align_bytes=64)
             nc.vector.quantize_mx(
                 out=lap_codes[:].bitcast(FP8X4),
                 scales=lap_scales[:],
-                in_=lap_grouped_of[(g, m)][:],
+                in_=lap_grouped_of[(g, first_m)][:],
             )
-            acc = psum_o.tile([P, FEATS], F32)
-            nc.tensor.matmul_mx(
-                out=acc[:],
-                lhsT=lap_codes[:].bitcast(FP8X4),
-                lhsT_scale=lap_scales[:],
-                rhs=x_codes_of[g][:].bitcast(FP8X4),
-                rhs_scale=x_scales_of[g][:],
-                start=True,
-                stop=True,
-            )
-            result = results.tile([P, FEATS], F32)
-            nc.scalar.copy(out=result[:], in_=acc[:])
-            nc.sync.dma_start(out=out[g, m * P : (m + 1) * P, :], in_=result[:])
+            for local in range(GROUP):
+                m = first_m + local
+                rows = slice(local * P, (local + 1) * P)
+                acc = psum_o.tile([P, FEATS], F32)
+                nc.tensor.matmul_mx(
+                    out=acc[:],
+                    lhsT=lap_codes[:, rows].bitcast(FP8X4),
+                    lhsT_scale=lap_scales[:, rows],
+                    rhs=x_codes_of[g][:].bitcast(FP8X4),
+                    rhs_scale=x_scales_of[g][:],
+                    start=True,
+                    stop=True,
+                )
+                result = results.tile([P, FEATS], F32)
+                nc.scalar.copy(out=result[:], in_=acc[:])
+                nc.sync.dma_start(out=out[g, m * P : (m + 1) * P, :], in_=result[:])
 
         load_adj(0)
         load_adj(1)
@@ -204,19 +233,21 @@ def tile_cheblayer_pa_kernel(tc, x, adj, out):
         for quarter in range(ROW_TILES):
             regroup_x(0, quarter)
 
-        for first in range(0, UNITS + LAG, GROUP):
-            for unit in range(first, min(first + GROUP, UNITS)):
-                g, m = divmod(unit, ROW_TILES)
-                laplacian(g, m)
-                if g + 2 < GRAPHS:
-                    row_sum(g + 2, m)
-                transpose_laplacian(g, m)
-                if g + 1 < GRAPHS:
-                    regroup_x(g + 1, m)
-                if m == 1:
-                    quantise_x(g)
-                if m == 2 and g + 1 < GRAPHS:
+        for first in range(0, UNITS + GROUP, GROUP):
+            if first < UNITS:
+                g, first_m = divmod(first, ROW_TILES)
+                laplacian(g, first_m)
+                for m in range(first_m, first_m + GROUP):
+                    if g + 2 < GRAPHS:
+                        row_sum(g + 2, m)
+                transpose_laplacian(g, first_m)
+                for m in range(first_m, first_m + GROUP):
+                    if g + 1 < GRAPHS:
+                        regroup_x(g + 1, m)
+                if first_m == 0 and g + 1 < GRAPHS:
                     inverse_roots(g + 1)
-            for unit in range(max(first - LAG, 0), first - LAG + GROUP):
-                g, m = divmod(unit, ROW_TILES)
-                multiply(g, m)
+                if first_m == GROUP:
+                    quantise_x(g)
+            if first >= GROUP:
+                g, first_m = divmod(first - GROUP, ROW_TILES)
+                multiply(g, first_m)

@@ -50,12 +50,12 @@ def tile_cheblayer_pa_kernel(tc, x, adj, out):
         eps = const.tile([P, 1], F32)
         nc.vector.memset(eps[:], EPS)
         table_warmer = const.tile([P, 1], F32)
-        nc.scalar.activation(out=table_warmer[:], in_=eps[:], func=ACT.Sqrt)
+        nc.scalar.activation(out=table_warmer[:], in_=eps[:], func=ACT.Abs_reciprocal_sqrt)
         eye_pair = psum_c.tile([P, GROUP, P], F32)
         for local in range(GROUP):
             nc.tensor.transpose(out=eye_pair[:, local, :], in_=eye_f32[:], identity=eye_f32[:])
 
-        adj_of, x_of, degree_of, root_of, r_neg_of, r_cols_of = {}, {}, {}, {}, {}, {}
+        adj_of, x_of, degree_of, r_pos_of, r_neg_of, r_cols_of = {}, {}, {}, {}, {}, {}
         x_grouped_of, x_codes_of, x_scales_of, lap_of, lap_grouped_of = {}, {}, {}, {}, {}
 
         def load_adj(g):
@@ -97,25 +97,27 @@ def tile_cheblayer_pa_kernel(tc, x, adj, out):
                 unread_s = per_unit.tile([P, NODES], BF16)
                 nc.scalar.activation(out=unread_s[:], in_=adj_of[g][:, m, :], func=ACT.Copy, accum_out=total)
             if m == ROW_TILES - 1:
-                root = per_graph.tile([P, ROW_TILES], F32)
+                r_pos = per_graph.tile([P, ROW_TILES], F32)
                 nc.scalar.activation(
-                    out=root[:], in_=degree_of[g][:, :, 0], func=ACT.Sqrt, bias=eps[:, 0:1], scale=1.0
+                    out=r_pos[:],
+                    in_=degree_of[g][:, :, 0],
+                    func=ACT.Abs_reciprocal_sqrt,
+                    bias=eps[:, 0:1],
+                    scale=1.0,
                 )
-                root_of[g] = root
+                r_neg = per_graph.tile([P, ROW_TILES], F32)
+                nc.scalar.mul(out=r_neg[:], in_=r_pos[:], mul=-1.0)
+                r_pos_of[g] = r_pos
+                r_neg_of[g] = r_neg
 
         def inverse_roots(g):
-            r_pos = per_graph.tile([P, ROW_TILES], F32)
-            nc.vector.reciprocal(out=r_pos[:], in_=root_of[g][:])
-            r_neg = per_graph.tile([P, ROW_TILES], F32)
-            nc.vector.tensor_scalar_mul(out=r_neg[:], in0=r_pos[:], scalar1=-1.0)
             r_cols = psum_r.tile([P, NODES], F32)
             for m in range(ROW_TILES):
                 nc.tensor.transpose(
                     out=r_cols[:, m * P : (m + 1) * P],
-                    in_=r_pos[:, m : m + 1].to_broadcast([P, P]),
+                    in_=r_pos_of[g][:, m : m + 1].to_broadcast([P, P]),
                     identity=eye_f32[:],
                 )
-            r_neg_of[g] = r_neg
             r_cols_of[g] = r_cols
 
         def regroup_x(g, quarter):

@@ -25,7 +25,7 @@ EPS = 1e-6
 GROUP = 2
 PITCH = NODES + P
 LAP_WIDTH = (ROW_TILES - GROUP) * P + GROUP * PITCH
-SCALAR_ALONE = 2
+SCALAR_ALONE = 0
 
 FLOPS = 2 * GRAPHS * NODES * NODES * FEATS
 
@@ -56,6 +56,7 @@ def tile_cheblayer_pa_kernel(tc, x, adj, out):
             nc.tensor.transpose(out=eye_pair[:, local, :], in_=eye_f32[:], identity=eye_f32[:])
 
         adj_of, x_of, degree_of, r_pos_of, r_neg_of, r_cols_of = {}, {}, {}, {}, {}, {}
+        scaled_of = {}
         x_grouped_of, x_codes_of, x_scales_of, lap_of, lap_grouped_of = {}, {}, {}, {}, {}
 
         def load_adj(g):
@@ -134,6 +135,10 @@ def tile_cheblayer_pa_kernel(tc, x, adj, out):
                 op1=ALU.add,
             )
 
+        def follow_vector(g, first_m):
+            seen = per_pair.tile([P, 1], F32)
+            nc.gpsimd.tensor_copy(out=seen[:], in_=scaled_of[(g, first_m)][:, 0, 0:1])
+
         def quantise_x(g):
             x_codes = per_graph.tile([P, FEATS], U32, align_bytes=64)
             x_scales = per_graph.tile([P, FEATS], U8, align_bytes=64)
@@ -177,6 +182,7 @@ def tile_cheblayer_pa_kernel(tc, x, adj, out):
                 op=ALU.add,
             )
             lap_of[(g, first_m)] = lap_pair
+            scaled_of[(g, first_m)] = scaled
 
         def transpose_laplacian(g, first_m):
             lap_words = lap_of[(g, first_m)][:, 0 : GROUP * NODES].bitcast(F32)
@@ -243,6 +249,8 @@ def tile_cheblayer_pa_kernel(tc, x, adj, out):
                     if g + 2 < GRAPHS:
                         row_sum(g + 2, m)
                 transpose_laplacian(g, first_m)
+                if g + 1 < GRAPHS:
+                    follow_vector(g, first_m)
                 for m in range(first_m, first_m + GROUP):
                     if g + 1 < GRAPHS:
                         regroup_x(g + 1, m)

@@ -56,7 +56,7 @@ def tile_cheblayer_pa_kernel(tc, x, adj, out):
             nc.tensor.transpose(out=eye_pair[:, local, :], in_=eye_f32[:], identity=eye_f32[:])
 
         adj_of, x_of, degree_of, r_pos_of, r_neg_of, r_cols_of = {}, {}, {}, {}, {}, {}
-        scaled_of = {}
+        lap_codes_of = {}
         x_grouped_of, x_codes_of, x_scales_of, lap_of, lap_grouped_of = {}, {}, {}, {}, {}
 
         def load_adj(g):
@@ -121,11 +121,11 @@ def tile_cheblayer_pa_kernel(tc, x, adj, out):
                 )
             r_cols_of[g] = r_cols
 
-        def regroup_x(g, quarter):
-            if quarter == 0:
+        def regroup_x(g, half):
+            if half == 0:
                 x_grouped = per_graph.tile([P, FEATS, PACK], BF16, align_bytes=64)
                 x_grouped_of[g] = x_grouped
-            cols = slice(quarter * P, (quarter + 1) * P)
+            cols = slice(half * FEATS // 2, (half + 1) * FEATS // 2)
             nc.gpsimd.tensor_scalar(
                 out=x_grouped_of[g][:, cols, :],
                 in0=x_of[g][:, :, cols].rearrange("p t f -> p f t"),
@@ -136,8 +136,8 @@ def tile_cheblayer_pa_kernel(tc, x, adj, out):
             )
 
         def follow_vector(g, first_m):
-            seen = per_pair.tile([P, 1], F32)
-            nc.gpsimd.tensor_copy(out=seen[:], in_=scaled_of[(g, first_m)][:, 0, 0:1])
+            seen = per_pair.tile([P, 1], U32)
+            nc.gpsimd.tensor_copy(out=seen[:], in_=lap_codes_of[(g, first_m)][:, 0:1])
 
         def quantise_x(g):
             x_codes = per_graph.tile([P, FEATS], U32, align_bytes=64)
@@ -182,7 +182,6 @@ def tile_cheblayer_pa_kernel(tc, x, adj, out):
                 op=ALU.add,
             )
             lap_of[(g, first_m)] = lap_pair
-            scaled_of[(g, first_m)] = scaled
 
         def transpose_laplacian(g, first_m):
             lap_words = lap_of[(g, first_m)][:, 0 : GROUP * NODES].bitcast(F32)
@@ -210,6 +209,7 @@ def tile_cheblayer_pa_kernel(tc, x, adj, out):
                 scales=lap_scales[:],
                 in_=lap_grouped_of[(g, first_m)][:],
             )
+            lap_codes_of[(g, first_m)] = lap_codes
             for local in range(GROUP):
                 m = first_m + local
                 rows = slice(local * P, (local + 1) * P)
@@ -238,8 +238,8 @@ def tile_cheblayer_pa_kernel(tc, x, adj, out):
             for m in range(ROW_TILES):
                 row_sum(g, m)
         inverse_roots(0)
-        for quarter in range(ROW_TILES):
-            regroup_x(0, quarter)
+        for half in range(2):
+            regroup_x(0, half)
 
         for first in range(0, UNITS + GROUP, GROUP):
             if first < UNITS:
@@ -250,10 +250,9 @@ def tile_cheblayer_pa_kernel(tc, x, adj, out):
                         row_sum(g + 2, m)
                 transpose_laplacian(g, first_m)
                 if g + 1 < GRAPHS:
-                    follow_vector(g, first_m)
-                for m in range(first_m, first_m + GROUP):
-                    if g + 1 < GRAPHS:
-                        regroup_x(g + 1, m)
+                    if first >= 2 * GROUP:
+                        follow_vector((first - 2 * GROUP) // ROW_TILES, (first - 2 * GROUP) % ROW_TILES)
+                    regroup_x(g + 1, first_m // GROUP)
                 if first_m == 0 and g + 1 < GRAPHS:
                     inverse_roots(g + 1)
                 if first_m == GROUP:

@@ -42,7 +42,7 @@ def tile_cheblayer_pa_kernel(tc, x, adj, out):
         results = ctx.enter_context(tc.tile_pool(name="results", bufs=UNITS))
         psum_r = ctx.enter_context(tc.psum_pool(name="psum_r", bufs=2))
         psum_t = ctx.enter_context(tc.psum_pool(name="psum_t", bufs=2))
-        psum_o = ctx.enter_context(tc.psum_pool(name="psum_o", bufs=GROUP))
+        psum_o = ctx.enter_context(tc.psum_pool(name="psum_o", bufs=GROUP + 1))
         psum_c = ctx.enter_context(tc.psum_pool(name="psum_c", bufs=1))
 
         eye_f32 = const.tile([P, P], F32)
@@ -56,24 +56,25 @@ def tile_cheblayer_pa_kernel(tc, x, adj, out):
             nc.tensor.transpose(out=eye_pair[:, local, :], in_=eye_f32[:], identity=eye_f32[:])
 
         adj_of, x_of, degree_of, r_pos_of, r_neg_of, r_cols_of = {}, {}, {}, {}, {}, {}
-        lap_codes_of = {}
+        lap_codes_of, lap_scales_of, acc_of = {}, {}, {}
         x_grouped_of, x_codes_of, x_scales_of, lap_of, lap_grouped_of = {}, {}, {}, {}, {}
 
         def load_adj(g):
             adj_sb = loads.tile([P, ROW_TILES, NODES], BF16)
-            nc.sync.dma_start(out=adj_sb[:], in_=adj[g].rearrange("(m p) j -> p m j", p=P))
+            if g == 0:
+                for m in range(ROW_TILES):
+                    nc.sync.dma_start(out=adj_sb[:, m, :], in_=adj[g, m * P : (m + 1) * P, :])
+            else:
+                nc.sync.dma_start(out=adj_sb[:], in_=adj[g].rearrange("(m p) j -> p m j", p=P))
             adj_of[g] = adj_sb
 
         def load_x(g):
             x_sb = loads.tile([P, PACK, FEATS], BF16)
-            nc.sync.dma_start(
-                out=x_sb[:].rearrange("p (u e) f -> p u e f", u=HALVES),
-                in_=x[g].rearrange("(u p e) f -> p u e f", u=HALVES, e=PAIR),
-            )
+            nc.sync.dma_start(out=x_sb[:], in_=x[g].rearrange("(p t) f -> p t f", t=PACK))
             x_of[g] = x_sb
 
         def row_sum(g, m):
-            if m == 0:
+            if g not in degree_of:
                 degree = per_graph.tile([P, ROW_TILES, OWN_BLOCK], F32)
                 degree_of[g] = degree
             total = degree_of[g][:, m, 0:1]
@@ -126,6 +127,9 @@ def tile_cheblayer_pa_kernel(tc, x, adj, out):
                 x_grouped = per_graph.tile([P, FEATS, PACK], BF16, align_bytes=64)
                 x_grouped_of[g] = x_grouped
             cols = slice(half * FEATS // 2, (half + 1) * FEATS // 2)
+            if g == 0 and half == 1:
+                nc.scalar.copy(out=x_grouped_of[g][:, cols, :], in_=x_of[g][:, :, cols].rearrange("p t f -> p f t"))
+                return
             nc.gpsimd.tensor_scalar(
                 out=x_grouped_of[g][:, cols, :],
                 in0=x_of[g][:, :, cols].rearrange("p t f -> p f t"),
@@ -191,7 +195,7 @@ def tile_cheblayer_pa_kernel(tc, x, adj, out):
                 for u in range(HALVES):
                     nc.tensor.transpose(
                         out=lap_t[:, u, local * P : (local + 1) * P],
-                        in_=lap_words[:, local * words + u * P : local * words + (u + 1) * P],
+                        in_=lap_words[:, local * words + u : (local + 1) * words : HALVES],
                         identity=eye_f32[:],
                     )
             lap_grouped = per_pair.tile([P, GROUP * P * PACK], BF16, align_bytes=64)
@@ -201,7 +205,7 @@ def tile_cheblayer_pa_kernel(tc, x, adj, out):
             )
             lap_grouped_of[(g, first_m)] = lap_grouped
 
-        def multiply(g, first_m):
+        def quantise_laplacian(g, first_m):
             lap_codes = per_pair.tile([P, GROUP * P], U32, align_bytes=64)
             lap_scales = per_pair.tile([P, GROUP * P], U8, align_bytes=64)
             nc.vector.quantize_mx(
@@ -210,22 +214,30 @@ def tile_cheblayer_pa_kernel(tc, x, adj, out):
                 in_=lap_grouped_of[(g, first_m)][:],
             )
             lap_codes_of[(g, first_m)] = lap_codes
-            for local in range(GROUP):
-                m = first_m + local
-                rows = slice(local * P, (local + 1) * P)
-                acc = psum_o.tile([P, FEATS], F32)
-                nc.tensor.matmul_mx(
-                    out=acc[:],
-                    lhsT=lap_codes[:, rows].bitcast(FP8X4),
-                    lhsT_scale=lap_scales[:, rows],
-                    rhs=x_codes_of[g][:].bitcast(FP8X4),
-                    rhs_scale=x_scales_of[g][:],
-                    start=True,
-                    stop=True,
-                )
-                result = results.tile([P, FEATS], F32)
-                nc.scalar.copy(out=result[:], in_=acc[:])
-                nc.sync.dma_start(out=out[g, m * P : (m + 1) * P, :], in_=result[:])
+            lap_scales_of[(g, first_m)] = lap_scales
+
+        def mx_pass(g, m):
+            first_m = m - m % GROUP
+            rows = slice((m - first_m) * P, (m - first_m + 1) * P)
+            acc = psum_o.tile([P, FEATS], F32)
+            nc.tensor.matmul_mx(
+                out=acc[:],
+                lhsT=lap_codes_of[(g, first_m)][:, rows].bitcast(FP8X4),
+                lhsT_scale=lap_scales_of[(g, first_m)][:, rows],
+                rhs=x_codes_of[g][:].bitcast(FP8X4),
+                rhs_scale=x_scales_of[g][:],
+                start=True,
+                stop=True,
+            )
+            acc_of[(g, m)] = acc
+
+        def store(g, m, on_vector):
+            result = results.tile([P, FEATS], F32)
+            if on_vector:
+                nc.vector.tensor_copy(out=result[:], in_=acc_of[(g, m)][:])
+            else:
+                nc.scalar.copy(out=result[:], in_=acc_of[(g, m)][:])
+            nc.sync.dma_start(out=out[g, m * P : (m + 1) * P, :], in_=result[:])
 
         load_adj(0)
         load_adj(1)
@@ -246,8 +258,10 @@ def tile_cheblayer_pa_kernel(tc, x, adj, out):
                 g, first_m = divmod(first, ROW_TILES)
                 laplacian(g, first_m)
                 for m in range(first_m, first_m + GROUP):
-                    if g + 2 < GRAPHS:
+                    if g + 2 < GRAPHS and (first, m) != (0, 0):
                         row_sum(g + 2, m)
+                    if (first, m) == (GROUP, GROUP):
+                        row_sum(2, 0)
                 transpose_laplacian(g, first_m)
                 if g + 1 < GRAPHS:
                     if first >= 2 * GROUP:
@@ -257,6 +271,22 @@ def tile_cheblayer_pa_kernel(tc, x, adj, out):
                     inverse_roots(g + 1)
                 if first_m == GROUP:
                     quantise_x(g)
-            if first >= GROUP:
+            if GROUP <= first < UNITS:
                 g, first_m = divmod(first - GROUP, ROW_TILES)
-                multiply(g, first_m)
+                quantise_laplacian(g, first_m)
+                mx_pass(g, first_m)
+                if first < UNITS - GROUP:
+                    store(g, first_m, False)
+                    mx_pass(g, first_m + 1)
+                    store(g, first_m + 1, False)
+                else:
+                    mx_pass(g, first_m + 1)
+                    store(g, first_m, False)
+            if first == UNITS:
+                g = GRAPHS - 1
+                quantise_laplacian(g, GROUP)
+                store(g, 1, True)
+                mx_pass(g, 2)
+                mx_pass(g, 3)
+                store(g, 2, False)
+                store(g, 3, True)

@@ -56,7 +56,7 @@ def tile_cheblayer_pa_kernel(tc, x, adj, out):
             nc.tensor.transpose(out=eye_pair[:, local, :], in_=eye_f32[:], identity=eye_f32[:])
 
         adj_of, x_of, degree_of, r_pos_of, r_neg_of, r_cols_of = {}, {}, {}, {}, {}, {}
-        lap_codes_of, lap_scales_of, acc_of = {}, {}, {}
+        lap_codes_of, lap_scales_of, acc_of, scaled_of = {}, {}, {}, {}
         x_grouped_of, x_codes_of, x_scales_of, lap_of, lap_grouped_of = {}, {}, {}, {}, {}
 
         def load_adj(g):
@@ -143,6 +143,10 @@ def tile_cheblayer_pa_kernel(tc, x, adj, out):
             seen = per_pair.tile([P, 1], U32)
             nc.gpsimd.tensor_copy(out=seen[:], in_=lap_codes_of[(g, first_m)][:, 0:1])
 
+        def follow_first_pair(g, first_m):
+            seen_first = per_pair.tile([P, 1], F32)
+            nc.gpsimd.tensor_copy(out=seen_first[:], in_=scaled_of[(g, first_m)][:, 0, 0:1])
+
         def quantise_x(g):
             x_codes = per_graph.tile([P, FEATS], U32, align_bytes=64)
             x_scales = per_graph.tile([P, FEATS], U8, align_bytes=64)
@@ -186,6 +190,7 @@ def tile_cheblayer_pa_kernel(tc, x, adj, out):
                 op=ALU.add,
             )
             lap_of[(g, first_m)] = lap_pair
+            scaled_of[(g, first_m)] = scaled
 
         def transpose_laplacian(g, first_m):
             lap_words = lap_of[(g, first_m)][:, 0 : GROUP * NODES].bitcast(F32)
@@ -263,10 +268,13 @@ def tile_cheblayer_pa_kernel(tc, x, adj, out):
                     if (first, m) == (GROUP, GROUP):
                         row_sum(2, 0)
                 transpose_laplacian(g, first_m)
-                if g + 1 < GRAPHS:
-                    if first >= 2 * GROUP:
+                share = first // GROUP - 1
+                if 0 <= share < 2 * (GRAPHS - 1):
+                    if share == 0:
+                        follow_first_pair(g, first_m)
+                    else:
                         follow_vector((first - 2 * GROUP) // ROW_TILES, (first - 2 * GROUP) % ROW_TILES)
-                    regroup_x(g + 1, first_m // GROUP)
+                    regroup_x(1 + share // 2, share % 2)
                 if first_m == 0 and g + 1 < GRAPHS:
                     inverse_roots(g + 1)
                 if first_m == GROUP:

@@ -246,10 +246,11 @@ def tile_cheblayer_pa_kernel(tc, x, adj, out):
 
         load_adj(0)
         load_adj(1)
-        for g in range(GRAPHS):
+        load_x(0)
+        for g in range(1, GRAPHS):
             load_x(g)
-            if g + 2 < GRAPHS:
-                load_adj(g + 2)
+            if g + 1 < GRAPHS:
+                load_adj(g + 1)
 
         for g in range(2):
             for m in range(ROW_TILES):

@@ -98,19 +98,22 @@ def tile_cheblayer_pa_kernel(tc, x, adj, out):
             else:
                 unread_s = per_unit.tile([P, NODES], BF16)
                 nc.scalar.activation(out=unread_s[:], in_=adj_of[g][:, m, :], func=ACT.Copy, accum_out=total)
-            if m == ROW_TILES - 1:
-                r_pos = per_graph.tile([P, ROW_TILES], F32)
-                nc.scalar.activation(
-                    out=r_pos[:],
-                    in_=degree_of[g][:, :, 0],
-                    func=ACT.Abs_reciprocal_sqrt,
-                    bias=eps[:, 0:1],
-                    scale=1.0,
-                )
-                r_neg = per_graph.tile([P, ROW_TILES], F32)
-                nc.scalar.mul(out=r_neg[:], in_=r_pos[:], mul=-1.0)
-                r_pos_of[g] = r_pos
-                r_neg_of[g] = r_neg
+
+        def root(g):
+            r_pos = per_graph.tile([P, ROW_TILES], F32)
+            nc.scalar.activation(
+                out=r_pos[:],
+                in_=degree_of[g][:, :, 0],
+                func=ACT.Abs_reciprocal_sqrt,
+                bias=eps[:, 0:1],
+                scale=1.0,
+            )
+            r_pos_of[g] = r_pos
+
+        def negate(g):
+            r_neg = per_graph.tile([P, ROW_TILES], F32)
+            nc.scalar.mul(out=r_neg[:], in_=r_pos_of[g][:], mul=-1.0)
+            r_neg_of[g] = r_neg
 
         def inverse_roots(g):
             r_cols = psum_r.tile([P, NODES], F32)
@@ -255,6 +258,8 @@ def tile_cheblayer_pa_kernel(tc, x, adj, out):
         for g in range(2):
             for m in range(ROW_TILES):
                 row_sum(g, m)
+            root(g)
+            negate(g)
         inverse_roots(0)
         for half in range(2):
             regroup_x(0, half)
@@ -269,6 +274,8 @@ def tile_cheblayer_pa_kernel(tc, x, adj, out):
                     if (first, m) == (GROUP, GROUP):
                         row_sum(2, 0)
                 transpose_laplacian(g, first_m)
+                if first_m == GROUP and g + 2 < GRAPHS:
+                    root(g + 2)
                 share = first // GROUP - 1
                 if 0 <= share < 2 * (GRAPHS - 1):
                     if share == 0:
@@ -286,6 +293,8 @@ def tile_cheblayer_pa_kernel(tc, x, adj, out):
                 mx_pass(g, first_m)
                 if first < UNITS - GROUP:
                     store(g, first_m, False)
+                    if first_m == 0 and g + 2 < GRAPHS:
+                        negate(g + 2)
                     mx_pass(g, first_m + 1)
                     store(g, first_m + 1, False)
                 else:

@@ -70,7 +70,10 @@ def tile_cheblayer_pa_kernel(tc, x, adj, out):
 
         def load_x(g):
             x_sb = loads.tile([P, PACK, FEATS], BF16)
-            nc.sync.dma_start(out=x_sb[:], in_=x[g].rearrange("(p t) f -> p t f", t=PACK))
+            nc.sync.dma_start(
+                out=x_sb[:].rearrange("p (u e) f -> p u e f", u=HALVES),
+                in_=x[g].rearrange("(u p e) f -> p u e f", u=HALVES, e=PAIR),
+            )
             x_of[g] = x_sb
 
         def row_sum(g, m):
@@ -203,7 +206,7 @@ def tile_cheblayer_pa_kernel(tc, x, adj, out):
                 for u in range(HALVES):
                     nc.tensor.transpose(
                         out=lap_t[:, u, local * P : (local + 1) * P],
-                        in_=lap_words[:, local * words + u : (local + 1) * words : HALVES],
+                        in_=lap_words[:, local * words + u * P : local * words + (u + 1) * P],
                         identity=eye_f32[:],
                     )
             lap_grouped = per_pair.tile([P, GROUP * P * PACK], BF16, align_bytes=64)

@@ -23,9 +23,12 @@ PAIR = 2
 OWN_BLOCK = 8
 EPS = 1e-6
 GROUP = 2
-PITCH = NODES + P
-LAP_WIDTH = (ROW_TILES - GROUP) * P + GROUP * PITCH
-SCALAR_ALONE = 0
+
+HALF = NODES // 2
+OUTER = (0, 3)
+PLACE_OF_BLOCK = (0, 2, 3, 1)
+DIAGONAL_BLOCK = ((0, 3), (3, 0))
+ROW_TILE = ((0, 3), (1, 2))
 
 FLOPS = 2 * GRAPHS * NODES * NODES * FEATS
 
@@ -40,9 +43,9 @@ def tile_cheblayer_pa_kernel(tc, x, adj, out):
         per_unit = ctx.enter_context(tc.tile_pool(name="per_unit", bufs=4))
         per_pair = ctx.enter_context(tc.tile_pool(name="per_pair", bufs=3))
         results = ctx.enter_context(tc.tile_pool(name="results", bufs=UNITS))
-        psum_r = ctx.enter_context(tc.psum_pool(name="psum_r", bufs=2))
+        psum_r = ctx.enter_context(tc.psum_pool(name="psum_r", bufs=1))
         psum_t = ctx.enter_context(tc.psum_pool(name="psum_t", bufs=2))
-        psum_o = ctx.enter_context(tc.psum_pool(name="psum_o", bufs=GROUP + 1))
+        psum_o = ctx.enter_context(tc.psum_pool(name="psum_o", bufs=2))
         psum_c = ctx.enter_context(tc.psum_pool(name="psum_c", bufs=1))
 
         eye_f32 = const.tile([P, P], F32)
@@ -51,21 +54,29 @@ def tile_cheblayer_pa_kernel(tc, x, adj, out):
         nc.vector.memset(eps[:], EPS)
         table_warmer = const.tile([P, 1], F32)
         nc.scalar.activation(out=table_warmer[:], in_=eps[:], func=ACT.Abs_reciprocal_sqrt)
+        eye_bf16 = const.tile([P, P], BF16)
+        nc.scalar.copy(out=eye_bf16[:], in_=eye_f32[:])
         eye_pair = psum_c.tile([P, GROUP, P], F32)
         for local in range(GROUP):
             nc.tensor.transpose(out=eye_pair[:, local, :], in_=eye_f32[:], identity=eye_f32[:])
 
         adj_of, x_of, degree_of, r_pos_of, r_neg_of, r_cols_of = {}, {}, {}, {}, {}, {}
-        lap_codes_of, lap_scales_of, acc_of, scaled_of = {}, {}, {}, {}
+        lap_codes_of, lap_scales_of, acc_of, scaled_of, block_sum_of = {}, {}, {}, {}, {}
         x_grouped_of, x_codes_of, x_scales_of, lap_of, lap_grouped_of = {}, {}, {}, {}, {}
 
         def load_adj(g):
             adj_sb = loads.tile([P, ROW_TILES, NODES], BF16)
+            rows = adj[g].rearrange("(m p) j -> p m j", p=P)
             if g == 0:
-                for m in range(ROW_TILES):
-                    nc.sync.dma_start(out=adj_sb[:, m, :], in_=adj[g, m * P : (m + 1) * P, :])
+                for place in range(GROUP):
+                    nc.sync.dma_start(out=adj_sb[:, place, :], in_=rows[:, OUTER[place], :])
             else:
-                nc.sync.dma_start(out=adj_sb[:], in_=adj[g].rearrange("(m p) j -> p m j", p=P))
+                nc.sync.dma_start(out=adj_sb[:, 0:GROUP, :], in_=rows[:, 0:ROW_TILES:3, :])
+            for half in range(HALVES):
+                nc.sync.dma_start(
+                    out=adj_sb[:, GROUP:ROW_TILES, half * HALF : (half + 1) * HALF],
+                    in_=rows[:, 1:3, (1 - half) * HALF : (2 - half) * HALF],
+                )
             adj_of[g] = adj_sb
 
         def load_x(g):
@@ -76,31 +87,50 @@ def tile_cheblayer_pa_kernel(tc, x, adj, out):
             )
             x_of[g] = x_sb
 
-        def row_sum(g, m):
+        def kind_of(g, place):
+            if g == 0:
+                return "VVVS"[place]
+            if g == 1:
+                return "VSVS"[place]
+            if g == 2 and place < GROUP:
+                return "VS"[place]
+            return "VPSP"[place]
+
+        def add_blocks(g, place):
+            block_sum = psum_c.tile([P, P], F32)
+            for b in range(ROW_TILES):
+                nc.tensor.matmul(
+                    out=block_sum[:],
+                    lhsT=eye_bf16[:],
+                    rhs=adj_of[g][:, place, b * P : (b + 1) * P],
+                    start=b == 0,
+                    stop=b == ROW_TILES - 1,
+                )
+            block_sum_of[(g, place)] = block_sum
+
+        def row_sum(g, place):
             if g not in degree_of:
                 degree = per_graph.tile([P, ROW_TILES, OWN_BLOCK], F32)
                 degree_of[g] = degree
-            total = degree_of[g][:, m, 0:1]
-            if g == 0:
-                on_vector = m < ROW_TILES - 1
-            elif g <= SCALAR_ALONE:
-                on_vector = False
-            else:
-                on_vector = m % GROUP == 0
-            if on_vector:
+            total = degree_of[g][:, place, 0:1]
+            kind = kind_of(g, place)
+            if kind == "V":
                 unread_v = per_unit.tile([P, NODES], BF16)
                 nc.vector.tensor_scalar(
                     out=unread_v[:],
-                    in0=adj_of[g][:, m, :],
+                    in0=adj_of[g][:, place, :],
                     scalar1=1.0,
                     scalar2=None,
                     op0=ALU.mult,
                     op1=ALU.add,
                     accum_out=total,
                 )
-            else:
+            elif kind == "S":
                 unread_s = per_unit.tile([P, NODES], BF16)
-                nc.scalar.activation(out=unread_s[:], in_=adj_of[g][:, m, :], func=ACT.Copy, accum_out=total)
+                nc.scalar.activation(out=unread_s[:], in_=adj_of[g][:, place, :], func=ACT.Copy, accum_out=total)
+            else:
+                unread_b = per_unit.tile([P, P], F32)
+                nc.scalar.activation(out=unread_b[:], in_=block_sum_of[(g, place)][:], func=ACT.Copy, accum_out=total)
 
         def root(g):
             r_pos = per_graph.tile([P, ROW_TILES], F32)
@@ -118,15 +148,21 @@ def tile_cheblayer_pa_kernel(tc, x, adj, out):
             nc.scalar.mul(out=r_neg[:], in_=r_pos_of[g][:], mul=-1.0)
             r_neg_of[g] = r_neg
 
-        def inverse_roots(g):
-            r_cols = psum_r.tile([P, NODES], F32)
-            for m in range(ROW_TILES):
+        def inverse_roots(g, pair):
+            if pair == 0:
+                r_cols_x = psum_r.tile([P, NODES], F32)
+                r_cols = r_cols_x
+            else:
+                r_cols_y = psum_r.tile([P, NODES], F32)
+                r_cols = r_cols_y
+            for b in range(ROW_TILES):
+                place = PLACE_OF_BLOCK[(b + 2 * pair) % ROW_TILES]
                 nc.tensor.transpose(
-                    out=r_cols[:, m * P : (m + 1) * P],
-                    in_=r_pos_of[g][:, m : m + 1].to_broadcast([P, P]),
+                    out=r_cols[:, b * P : (b + 1) * P],
+                    in_=r_pos_of[g][:, place : place + 1].to_broadcast([P, P]),
                     identity=eye_f32[:],
                 )
-            r_cols_of[g] = r_cols
+            r_cols_of[(g, pair)] = r_cols
 
         def regroup_x(g, half):
             if half == 0:
@@ -145,13 +181,13 @@ def tile_cheblayer_pa_kernel(tc, x, adj, out):
                 op1=ALU.add,
             )
 
-        def follow_vector(g, first_m):
+        def follow_vector(g, pair):
             seen = per_pair.tile([P, 1], U32)
-            nc.gpsimd.tensor_copy(out=seen[:], in_=lap_codes_of[(g, first_m)][:, 0:1])
+            nc.gpsimd.tensor_copy(out=seen[:], in_=lap_codes_of[(g, pair)][:, 0:1])
 
-        def follow_first_pair(g, first_m):
+        def follow_first_pair(g, pair):
             seen_first = per_pair.tile([P, 1], F32)
-            nc.gpsimd.tensor_copy(out=seen_first[:], in_=scaled_of[(g, first_m)][:, 0, 0:1])
+            nc.gpsimd.tensor_copy(out=seen_first[:], in_=scaled_of[(g, pair)][:, 0, 0:1])
 
         def quantise_x(g):
             x_codes = per_graph.tile([P, FEATS], U32, align_bytes=64)
@@ -164,49 +200,50 @@ def tile_cheblayer_pa_kernel(tc, x, adj, out):
             x_codes_of[g] = x_codes
             x_scales_of[g] = x_scales
 
-        def scale_columns(g, m, cols, dest):
+        def scale_columns(g, pair, local, cols, dest):
+            place = GROUP * pair + local
             nc.vector.scalar_tensor_tensor(
                 out=dest,
-                in0=adj_of[g][:, m, cols],
-                scalar=r_neg_of[g][:, m : m + 1],
-                in1=r_cols_of[g][:, cols],
+                in0=adj_of[g][:, place, cols],
+                scalar=r_neg_of[g][:, place : place + 1],
+                in1=r_cols_of[(g, pair)][:, cols],
                 op0=ALU.mult,
                 op1=ALU.mult,
             )
 
-        def laplacian(g, first_m):
-            lap_pair = per_pair.tile([P, LAP_WIDTH], BF16)
+        def laplacian(g, pair):
+            lap_pair = per_pair.tile([P, GROUP * NODES], BF16)
             scaled = per_pair.tile([P, GROUP, P], F32)
             for local in range(GROUP):
-                m = first_m + local
-                scale_columns(g, m, slice(m * P, (m + 1) * P), scaled[:, local, :])
+                b = DIAGONAL_BLOCK[pair][local]
+                scale_columns(g, pair, local, slice(b * P, (b + 1) * P), scaled[:, local, :])
             for local in range(GROUP):
-                m = first_m + local
-                lap = lap_pair[:, local * NODES : (local + 1) * NODES]
-                if m > 0:
-                    scale_columns(g, m, slice(0, m * P), lap[:, 0 : m * P])
-                if m < ROW_TILES - 1:
-                    scale_columns(g, m, slice((m + 1) * P, NODES), lap[:, (m + 1) * P : NODES])
+                off = slice(P, NODES) if DIAGONAL_BLOCK[pair][local] == 0 else slice(0, NODES - P)
+                scale_columns(
+                    g, pair, local, off, lap_pair[:, local * NODES + off.start : local * NODES + off.stop]
+                )
+            blocks = lap_pair[:].rearrange("p (k c) -> p k c", c=P)
+            first = DIAGONAL_BLOCK[pair][0]
+            step = ROW_TILES + DIAGONAL_BLOCK[pair][1] - first
             nc.vector.tensor_tensor(
-                out=lap_pair[:, first_m * P : first_m * P + GROUP * PITCH].rearrange("p (l w) -> p l w", w=PITCH)[
-                    :, :, 0:P
-                ],
+                out=blocks[:, first : first + step + 1 : step, :],
                 in0=scaled[:],
                 in1=eye_pair[:],
                 op=ALU.add,
             )
-            lap_of[(g, first_m)] = lap_pair
-            scaled_of[(g, first_m)] = scaled
+            lap_of[(g, pair)] = lap_pair
+            scaled_of[(g, pair)] = scaled
 
-        def transpose_laplacian(g, first_m):
-            lap_words = lap_of[(g, first_m)][:, 0 : GROUP * NODES].bitcast(F32)
+        def transpose_laplacian(g, pair):
+            lap_words = lap_of[(g, pair)][:].bitcast(F32)
             words = NODES // PAIR
             lap_t = psum_t.tile([P, HALVES, GROUP * P], F32)
             for local in range(GROUP):
                 for u in range(HALVES):
+                    start = local * words + (u + pair) % HALVES * P
                     nc.tensor.transpose(
                         out=lap_t[:, u, local * P : (local + 1) * P],
-                        in_=lap_words[:, local * words + u * P : local * words + (u + 1) * P],
+                        in_=lap_words[:, start : start + P],
                         identity=eye_f32[:],
                     )
             lap_grouped = per_pair.tile([P, GROUP * P * PACK], BF16, align_bytes=64)
@@ -214,40 +251,40 @@ def tile_cheblayer_pa_kernel(tc, x, adj, out):
                 out=lap_grouped[:].bitcast(F32).rearrange("p (c u) -> p c u", u=HALVES),
                 in_=lap_t[:].rearrange("p u c -> p c u"),
             )
-            lap_grouped_of[(g, first_m)] = lap_grouped
+            lap_grouped_of[(g, pair)] = lap_grouped
 
-        def quantise_laplacian(g, first_m):
+        def quantise_laplacian(g, pair):
             lap_codes = per_pair.tile([P, GROUP * P], U32, align_bytes=64)
             lap_scales = per_pair.tile([P, GROUP * P], U8, align_bytes=64)
             nc.vector.quantize_mx(
                 out=lap_codes[:].bitcast(FP8X4),
                 scales=lap_scales[:],
-                in_=lap_grouped_of[(g, first_m)][:],
+                in_=lap_grouped_of[(g, pair)][:],
             )
-            lap_codes_of[(g, first_m)] = lap_codes
-            lap_scales_of[(g, first_m)] = lap_scales
+            lap_codes_of[(g, pair)] = lap_codes
+            lap_scales_of[(g, pair)] = lap_scales
 
-        def mx_pass(g, m):
-            first_m = m - m % GROUP
-            rows = slice((m - first_m) * P, (m - first_m + 1) * P)
+        def mx_pass(g, pair, local):
+            rows = slice(local * P, (local + 1) * P)
             acc = psum_o.tile([P, FEATS], F32)
             nc.tensor.matmul_mx(
                 out=acc[:],
-                lhsT=lap_codes_of[(g, first_m)][:, rows].bitcast(FP8X4),
-                lhsT_scale=lap_scales_of[(g, first_m)][:, rows],
+                lhsT=lap_codes_of[(g, pair)][:, rows].bitcast(FP8X4),
+                lhsT_scale=lap_scales_of[(g, pair)][:, rows],
                 rhs=x_codes_of[g][:].bitcast(FP8X4),
                 rhs_scale=x_scales_of[g][:],
                 start=True,
                 stop=True,
             )
-            acc_of[(g, m)] = acc
+            acc_of[(g, pair, local)] = acc
 
-        def store(g, m, on_vector):
+        def store(g, pair, local, on_vector):
+            m = ROW_TILE[pair][local]
             result = results.tile([P, FEATS], F32)
             if on_vector:
-                nc.vector.tensor_copy(out=result[:], in_=acc_of[(g, m)][:])
+                nc.vector.tensor_copy(out=result[:], in_=acc_of[(g, pair, local)][:])
             else:
-                nc.scalar.copy(out=result[:], in_=acc_of[(g, m)][:])
+                nc.scalar.copy(out=result[:], in_=acc_of[(g, pair, local)][:])
             nc.sync.dma_start(out=out[g, m * P : (m + 1) * P, :], in_=result[:])
 
         load_adj(0)
@@ -259,55 +296,63 @@ def tile_cheblayer_pa_kernel(tc, x, adj, out):
                 load_adj(g + 1)
 
         for g in range(2):
-            for m in range(ROW_TILES):
-                row_sum(g, m)
+            for place in range(ROW_TILES):
+                row_sum(g, place)
             root(g)
             negate(g)
-        inverse_roots(0)
+            if g == 0:
+                inverse_roots(0, 0)
         for half in range(2):
             regroup_x(0, half)
 
-        for first in range(0, UNITS + GROUP, GROUP):
-            if first < UNITS:
-                g, first_m = divmod(first, ROW_TILES)
-                laplacian(g, first_m)
-                for m in range(first_m, first_m + GROUP):
-                    if g + 2 < GRAPHS and (first, m) != (0, 0):
-                        row_sum(g + 2, m)
-                    if (first, m) == (GROUP, GROUP):
-                        row_sum(2, 0)
-                transpose_laplacian(g, first_m)
-                if first_m == GROUP and g + 2 < GRAPHS:
+        STEPS = 2 * GRAPHS
+        for step in range(STEPS + 1):
+            if step < STEPS:
+                g, pair = divmod(step, 2)
+                laplacian(g, pair)
+                if step + 1 < STEPS:
+                    inverse_roots((step + 1) // 2, (step + 1) % 2)
+                if g + 2 < GRAPHS:
+                    for place in range(GROUP * pair, GROUP * pair + GROUP):
+                        if (step, place) != (0, 0):
+                            row_sum(g + 2, place)
+                        if (step, place) == (1, 2):
+                            row_sum(2, 0)
+                transpose_laplacian(g, pair)
+                if pair == 1 and g + 2 < GRAPHS:
                     root(g + 2)
-                share = first // GROUP - 1
+                share = step - 1
                 if 0 <= share < 2 * (GRAPHS - 1):
                     if share == 0:
-                        follow_first_pair(g, first_m)
+                        follow_first_pair(g, pair)
                     else:
-                        follow_vector((first - 2 * GROUP) // ROW_TILES, (first - 2 * GROUP) % ROW_TILES)
+                        follow_vector((step - 2) // 2, step % 2)
                     regroup_x(1 + share // 2, share % 2)
-                if first_m == 0 and g + 1 < GRAPHS:
-                    inverse_roots(g + 1)
-                if first_m == GROUP:
+                if pair == 1:
                     quantise_x(g)
-            if GROUP <= first < UNITS:
-                g, first_m = divmod(first - GROUP, ROW_TILES)
-                quantise_laplacian(g, first_m)
-                mx_pass(g, first_m)
-                if first < UNITS - GROUP:
-                    store(g, first_m, False)
-                    if first_m == 0 and g + 2 < GRAPHS:
+            if 1 <= step < STEPS:
+                g, pair = divmod(step - 1, 2)
+                quantise_laplacian(g, pair)
+                mx_pass(g, pair, 0)
+                if step < STEPS - 1:
+                    store(g, pair, 0, False)
+                    if pair == 0 and g + 2 < GRAPHS:
                         negate(g + 2)
-                    mx_pass(g, first_m + 1)
-                    store(g, first_m + 1, False)
+                    mx_pass(g, pair, 1)
+                    store(g, pair, 1, False)
                 else:
-                    mx_pass(g, first_m + 1)
-                    store(g, first_m, False)
-            if first == UNITS:
+                    mx_pass(g, pair, 1)
+                    store(g, pair, 0, False)
+            if step + 1 < STEPS:
+                g, pair = divmod(step + 1, 2)
+                for place in range(GROUP * pair, GROUP * pair + GROUP):
+                    if g + 2 < GRAPHS and kind_of(g + 2, place) == "P":
+                        add_blocks(g + 2, place)
+            if step == STEPS:
                 g = GRAPHS - 1
-                quantise_laplacian(g, GROUP)
-                store(g, 1, True)
-                mx_pass(g, 2)
-                mx_pass(g, 3)
-                store(g, 2, False)
-                store(g, 3, True)
+                quantise_laplacian(g, 1)
+                store(g, 0, 1, True)
+                mx_pass(g, 1, 0)
+                mx_pass(g, 1, 1)
+                store(g, 1, 0, False)
+                store(g, 1, 1, True)

@@ -168,7 +168,10 @@ def tile_cheblayer_pa_kernel(tc, x, adj, out):
             if half == 0:
                 x_grouped = per_graph.tile([P, FEATS, PACK], BF16, align_bytes=64)
                 x_grouped_of[g] = x_grouped
-            cols = slice(half * FEATS // 2, (half + 1) * FEATS // 2)
+            if g == 0:
+                cols = slice(half * FEATS // 2, (half + 1) * FEATS // 2)
+            else:
+                cols = slice(0, 192) if half == 0 else slice(192, 448)
             if g == 0 and half == 1:
                 nc.scalar.copy(out=x_grouped_of[g][:, cols, :], in_=x_of[g][:, :, cols].rearrange("p t f -> p f t"))
                 return
@@ -180,6 +183,10 @@ def tile_cheblayer_pa_kernel(tc, x, adj, out):
                 op0=ALU.mult,
                 op1=ALU.add,
             )
+
+        def regroup_rest(g):
+            rest = slice(448, FEATS)
+            nc.scalar.copy(out=x_grouped_of[g][:, rest, :], in_=x_of[g][:, :, rest].rearrange("p t f -> p f t"))
 
         def follow_vector(g, pair):
             seen = per_pair.tile([P, 1], U32)
@@ -312,6 +319,8 @@ def tile_cheblayer_pa_kernel(tc, x, adj, out):
                 laplacian(g, pair)
                 if step + 1 < STEPS:
                     inverse_roots((step + 1) // 2, (step + 1) % 2)
+                if pair == 0 and 0 < g:
+                    regroup_rest(g)
                 if g + 2 < GRAPHS:
                     for place in range(GROUP * pair, GROUP * pair + GROUP):
                         if (step, place) != (0, 0):

@@ -16,19 +16,21 @@ GRAPHS = 8
 NODES = 512
 FEATS = 512
 ROW_TILES = NODES // P
-UNITS = GRAPHS * ROW_TILES
 PACK = 4
 HALVES = 2
+HALF = NODES // HALVES
 PAIR = 2
 OWN_BLOCK = 8
 EPS = 1e-6
 GROUP = 2
-
-HALF = NODES // 2
-OUTER = (0, 3)
-PLACE_OF_BLOCK = (0, 2, 3, 1)
-DIAGONAL_BLOCK = ((0, 3), (3, 0))
+OUTER, INNER = 0, 1
+STEPS = 2 * GRAPHS
+BOTH = (0, 1)
 ROW_TILE = ((0, 3), (1, 2))
+DIAGONAL_BLOCK = ((0, 3), (3, 0))
+PLACE_OF_BLOCK = (0, 2, 3, 1)
+RUN = 4
+GPSIMD_FIRST = 224
 
 FLOPS = 2 * GRAPHS * NODES * NODES * FEATS
 
@@ -42,7 +44,7 @@ def tile_cheblayer_pa_kernel(tc, x, adj, out):
         per_graph = ctx.enter_context(tc.tile_pool(name="per_graph", bufs=3))
         per_unit = ctx.enter_context(tc.tile_pool(name="per_unit", bufs=4))
         per_pair = ctx.enter_context(tc.tile_pool(name="per_pair", bufs=3))
-        results = ctx.enter_context(tc.tile_pool(name="results", bufs=UNITS))
+        results = ctx.enter_context(tc.tile_pool(name="results", bufs=GRAPHS * ROW_TILES))
         psum_r = ctx.enter_context(tc.psum_pool(name="psum_r", bufs=1))
         psum_t = ctx.enter_context(tc.psum_pool(name="psum_t", bufs=2))
         psum_o = ctx.enter_context(tc.psum_pool(name="psum_o", bufs=2))
@@ -57,7 +59,7 @@ def tile_cheblayer_pa_kernel(tc, x, adj, out):
         eye_bf16 = const.tile([P, P], BF16)
         nc.scalar.copy(out=eye_bf16[:], in_=eye_f32[:])
         eye_pair = psum_c.tile([P, GROUP, P], F32)
-        for local in range(GROUP):
+        for local in BOTH:
             nc.tensor.transpose(out=eye_pair[:, local, :], in_=eye_f32[:], identity=eye_f32[:])
 
         adj_of, x_of, degree_of, r_pos_of, r_neg_of, r_cols_of = {}, {}, {}, {}, {}, {}
@@ -68,8 +70,8 @@ def tile_cheblayer_pa_kernel(tc, x, adj, out):
             adj_sb = loads.tile([P, ROW_TILES, NODES], BF16)
             rows = adj[g].rearrange("(m p) j -> p m j", p=P)
             if g == 0:
-                for place in range(GROUP):
-                    nc.sync.dma_start(out=adj_sb[:, place, :], in_=rows[:, OUTER[place], :])
+                for local in BOTH:
+                    nc.sync.dma_start(out=adj_sb[:, local, :], in_=rows[:, ROW_TILE[OUTER][local], :])
             else:
                 nc.sync.dma_start(out=adj_sb[:, 0:GROUP, :], in_=rows[:, 0:ROW_TILES:3, :])
             for half in range(HALVES):
@@ -87,17 +89,15 @@ def tile_cheblayer_pa_kernel(tc, x, adj, out):
             )
             x_of[g] = x_sb
 
-        def kind_of(g, place):
+        def summed_by(g, place):
             if g == 0:
                 return "VVVS"[place]
-            if g == 1:
+            if g == 1 or (g == 2 and place < GROUP):
                 return "VSVS"[place]
-            if g == 2 and place < GROUP:
-                return "VS"[place]
-            return "VPSP"[place]
+            return "VBSB"[place]
 
         def add_blocks(g, place):
-            block_sum = psum_c.tile([P, P], F32)
+            block_sum = psum_c.tile([P, P], F32, name="spare")
             for b in range(ROW_TILES):
                 nc.tensor.matmul(
                     out=block_sum[:],
@@ -113,8 +113,8 @@ def tile_cheblayer_pa_kernel(tc, x, adj, out):
                 degree = per_graph.tile([P, ROW_TILES, OWN_BLOCK], F32)
                 degree_of[g] = degree
             total = degree_of[g][:, place, 0:1]
-            kind = kind_of(g, place)
-            if kind == "V":
+            engine = summed_by(g, place)
+            if engine == "V":
                 unread_v = per_unit.tile([P, NODES], BF16)
                 nc.vector.tensor_scalar(
                     out=unread_v[:],
@@ -125,7 +125,7 @@ def tile_cheblayer_pa_kernel(tc, x, adj, out):
                     op1=ALU.add,
                     accum_out=total,
                 )
-            elif kind == "S":
+            elif engine == "S":
                 unread_s = per_unit.tile([P, NODES], BF16)
                 nc.scalar.activation(out=unread_s[:], in_=adj_of[g][:, place, :], func=ACT.Copy, accum_out=total)
             else:
@@ -148,13 +148,13 @@ def tile_cheblayer_pa_kernel(tc, x, adj, out):
             nc.scalar.mul(out=r_neg[:], in_=r_pos_of[g][:], mul=-1.0)
             r_neg_of[g] = r_neg
 
-        def inverse_roots(g, pair):
-            if pair == 0:
-                r_cols_x = psum_r.tile([P, NODES], F32)
-                r_cols = r_cols_x
+        def spread_roots(g, pair):
+            if pair == OUTER:
+                r_cols_outer = psum_r.tile([P, NODES], F32, name="r_cols_outer")
+                r_cols = r_cols_outer
             else:
-                r_cols_y = psum_r.tile([P, NODES], F32)
-                r_cols = r_cols_y
+                r_cols_inner = psum_r.tile([P, NODES], F32)
+                r_cols = r_cols_inner
             for b in range(ROW_TILES):
                 place = PLACE_OF_BLOCK[(b + 2 * pair) % ROW_TILES]
                 nc.tensor.transpose(
@@ -164,33 +164,32 @@ def tile_cheblayer_pa_kernel(tc, x, adj, out):
                 )
             r_cols_of[(g, pair)] = r_cols
 
-        def regroup_x(g, half):
-            if half == 0:
-                x_grouped = per_graph.tile([P, FEATS, PACK], BF16, align_bytes=64)
-                x_grouped_of[g] = x_grouped
-            if g == 0:
-                cols = slice(half * FEATS // 2, (half + 1) * FEATS // 2)
-            else:
-                cols = slice(0, 192) if half == 0 else slice(192, 448)
-            if g == 0 and half == 1:
-                nc.scalar.copy(out=x_grouped_of[g][:, cols, :], in_=x_of[g][:, :, cols].rearrange("p t f -> p f t"))
-                return
+        def new_x_grouped(g):
+            x_grouped = per_graph.tile([P, FEATS, PACK], BF16, align_bytes=64)
+            x_grouped_of[g] = x_grouped
+
+        def regroup_on_gpsimd(g, cols):
             nc.gpsimd.tensor_scalar(
-                out=x_grouped_of[g][:, cols, :],
-                in0=x_of[g][:, :, cols].rearrange("p t f -> p f t"),
+                out=x_grouped_of[g][:, cols, :].rearrange("p (c i) t -> p c t i", i=RUN),
+                in0=x_of[g][:, :, cols].rearrange("p t (c i) -> p c t i", i=RUN),
                 scalar1=1.0,
                 scalar2=0.0,
                 op0=ALU.mult,
                 op1=ALU.add,
             )
 
-        def regroup_rest(g):
-            rest = slice(448, FEATS)
-            nc.scalar.copy(out=x_grouped_of[g][:, rest, :], in_=x_of[g][:, :, rest].rearrange("p t f -> p f t"))
+        def regroup_on_scalar(g, cols):
+            nc.scalar.copy(
+                out=x_grouped_of[g][:, cols, :].rearrange("p (c i) t -> p c t i", i=RUN),
+                in_=x_of[g][:, :, cols].rearrange("p t (c i) -> p c t i", i=RUN),
+            )
+
+        def scalar_first(g):
+            return FEATS - (0 if g + 2 < GRAPHS else 128)
 
         def follow_vector(g, pair):
             seen = per_pair.tile([P, 1], U32)
-            nc.gpsimd.tensor_copy(out=seen[:], in_=lap_codes_of[(g, pair)][:, 0:1])
+            nc.gpsimd.tensor_copy(out=seen[:], in_=lap_codes_of[(g, pair, 0)][:, 0:1])
 
         def follow_first_pair(g, pair):
             seen_first = per_pair.tile([P, 1], F32)
@@ -207,6 +206,12 @@ def tile_cheblayer_pa_kernel(tc, x, adj, out):
             x_codes_of[g] = x_codes
             x_scales_of[g] = x_scales
 
+        def new_laplacian(g, pair):
+            lap_pair = per_pair.tile([P, GROUP * ROW_TILES, P], BF16)
+            scaled = per_pair.tile([P, GROUP, P], F32)
+            lap_of[(g, pair)] = lap_pair
+            scaled_of[(g, pair)] = scaled
+
         def scale_columns(g, pair, local, cols, dest):
             place = GROUP * pair + local
             nc.vector.scalar_tensor_tensor(
@@ -218,66 +223,64 @@ def tile_cheblayer_pa_kernel(tc, x, adj, out):
                 op1=ALU.mult,
             )
 
-        def laplacian(g, pair):
-            lap_pair = per_pair.tile([P, GROUP * NODES], BF16)
-            scaled = per_pair.tile([P, GROUP, P], F32)
-            for local in range(GROUP):
-                b = DIAGONAL_BLOCK[pair][local]
-                scale_columns(g, pair, local, slice(b * P, (b + 1) * P), scaled[:, local, :])
-            for local in range(GROUP):
-                off = slice(P, NODES) if DIAGONAL_BLOCK[pair][local] == 0 else slice(0, NODES - P)
-                scale_columns(
-                    g, pair, local, off, lap_pair[:, local * NODES + off.start : local * NODES + off.stop]
-                )
-            blocks = lap_pair[:].rearrange("p (k c) -> p k c", c=P)
-            first = DIAGONAL_BLOCK[pair][0]
-            step = ROW_TILES + DIAGONAL_BLOCK[pair][1] - first
+        def form_diagonal(g, pair, local):
+            b = DIAGONAL_BLOCK[pair][local]
+            scale_columns(g, pair, local, slice(b * P, (b + 1) * P), scaled_of[(g, pair)][:, local, :])
+
+        def form_rest(g, pair, local):
+            first = 1 if DIAGONAL_BLOCK[pair][local] == 0 else 0
+            blocks = lap_of[(g, pair)][:, local * ROW_TILES + first : local * ROW_TILES + first + ROW_TILES - 1, :]
+            cols = slice(first * P, (first + ROW_TILES - 1) * P)
+            scale_columns(g, pair, local, cols, blocks.rearrange("p b c -> p (b c)"))
+
+        def add_eye(g, pair, tiles):
+            first = tiles[0] * ROW_TILES + DIAGONAL_BLOCK[pair][tiles[0]]
+            last = tiles[-1] * ROW_TILES + DIAGONAL_BLOCK[pair][tiles[-1]]
             nc.vector.tensor_tensor(
-                out=blocks[:, first : first + step + 1 : step, :],
-                in0=scaled[:],
-                in1=eye_pair[:],
+                out=lap_of[(g, pair)][:, first : last + 1 : max(last - first, 1), :],
+                in0=scaled_of[(g, pair)][:, tiles[0] : tiles[-1] + 1, :],
+                in1=eye_pair[:, tiles[0] : tiles[-1] + 1, :],
                 op=ALU.add,
             )
-            lap_of[(g, pair)] = lap_pair
-            scaled_of[(g, pair)] = scaled
 
-        def transpose_laplacian(g, pair):
-            lap_words = lap_of[(g, pair)][:].bitcast(F32)
+        def transpose_laplacian(g, pair, tiles):
+            rows = lap_of[(g, pair)][:].rearrange("p b c -> p (b c)").bitcast(F32)
             words = NODES // PAIR
-            lap_t = psum_t.tile([P, HALVES, GROUP * P], F32)
-            for local in range(GROUP):
+            width = len(tiles) * P
+            lap_t = psum_t.tile([P, HALVES, width], F32, name="lap_t")
+            for local in tiles:
+                at = (local - tiles[0]) * P
                 for u in range(HALVES):
                     start = local * words + (u + pair) % HALVES * P
                     nc.tensor.transpose(
-                        out=lap_t[:, u, local * P : (local + 1) * P],
-                        in_=lap_words[:, start : start + P],
-                        identity=eye_f32[:],
+                        out=lap_t[:, u, at : at + P], in_=rows[:, start : start + P], identity=eye_f32[:]
                     )
-            lap_grouped = per_pair.tile([P, GROUP * P * PACK], BF16, align_bytes=64)
+            lap_grouped = per_pair.tile([P, width * PACK], BF16, align_bytes=64, name="lap_grouped")
             nc.scalar.copy(
                 out=lap_grouped[:].bitcast(F32).rearrange("p (c u) -> p c u", u=HALVES),
                 in_=lap_t[:].rearrange("p u c -> p c u"),
             )
-            lap_grouped_of[(g, pair)] = lap_grouped
+            lap_grouped_of[(g, pair, tiles[0])] = lap_grouped
 
-        def quantise_laplacian(g, pair):
-            lap_codes = per_pair.tile([P, GROUP * P], U32, align_bytes=64)
-            lap_scales = per_pair.tile([P, GROUP * P], U8, align_bytes=64)
+        def quantise_laplacian(g, pair, tiles):
+            width = len(tiles) * P
+            lap_codes = per_pair.tile([P, width], U32, align_bytes=64, name="lap_codes")
+            lap_scales = per_pair.tile([P, width], U8, align_bytes=64, name="lap_scales")
             nc.vector.quantize_mx(
                 out=lap_codes[:].bitcast(FP8X4),
                 scales=lap_scales[:],
-                in_=lap_grouped_of[(g, pair)][:],
+                in_=lap_grouped_of[(g, pair, tiles[0])][:],
             )
-            lap_codes_of[(g, pair)] = lap_codes
-            lap_scales_of[(g, pair)] = lap_scales
+            for local in tiles:
+                at = (local - tiles[0]) * P
+                lap_codes_of[(g, pair, local)] = lap_codes[:, at : at + P]
+                lap_scales_of[(g, pair, local)] = lap_scales[:, at : at + P]
 
-        def mx_pass(g, pair, local):
-            rows = slice(local * P, (local + 1) * P)
-            acc = psum_o.tile([P, FEATS], F32)
+        def mx_pass(g, pair, local, acc):
             nc.tensor.matmul_mx(
                 out=acc[:],
-                lhsT=lap_codes_of[(g, pair)][:, rows].bitcast(FP8X4),
-                lhsT_scale=lap_scales_of[(g, pair)][:, rows],
+                lhsT=lap_codes_of[(g, pair, local)].bitcast(FP8X4),
+                lhsT_scale=lap_scales_of[(g, pair, local)],
                 rhs=x_codes_of[g][:].bitcast(FP8X4),
                 rhs_scale=x_scales_of[g][:],
                 start=True,
@@ -308,60 +311,76 @@ def tile_cheblayer_pa_kernel(tc, x, adj, out):
             root(g)
             negate(g)
             if g == 0:
-                inverse_roots(0, 0)
-        for half in range(2):
-            regroup_x(0, half)
+                spread_roots(0, OUTER)
+        new_x_grouped(0)
+        regroup_on_gpsimd(0, slice(0, FEATS // 2))
+        regroup_on_scalar(0, slice(FEATS // 2, FEATS))
 
-        STEPS = 2 * GRAPHS
-        for step in range(STEPS + 1):
-            if step < STEPS:
-                g, pair = divmod(step, 2)
-                laplacian(g, pair)
-                if step + 1 < STEPS:
-                    inverse_roots((step + 1) // 2, (step + 1) % 2)
-                if pair == 0 and 0 < g:
-                    regroup_rest(g)
-                if g + 2 < GRAPHS:
-                    for place in range(GROUP * pair, GROUP * pair + GROUP):
-                        if (step, place) != (0, 0):
-                            row_sum(g + 2, place)
-                        if (step, place) == (1, 2):
-                            row_sum(2, 0)
-                transpose_laplacian(g, pair)
-                if pair == 1 and g + 2 < GRAPHS:
-                    root(g + 2)
-                share = step - 1
-                if 0 <= share < 2 * (GRAPHS - 1):
-                    if share == 0:
-                        follow_first_pair(g, pair)
-                    else:
-                        follow_vector((step - 2) // 2, step % 2)
-                    regroup_x(1 + share // 2, share % 2)
-                if pair == 1:
-                    quantise_x(g)
-            if 1 <= step < STEPS:
-                g, pair = divmod(step - 1, 2)
-                quantise_laplacian(g, pair)
-                mx_pass(g, pair, 0)
-                if step < STEPS - 1:
-                    store(g, pair, 0, False)
-                    if pair == 0 and g + 2 < GRAPHS:
-                        negate(g + 2)
-                    mx_pass(g, pair, 1)
-                    store(g, pair, 1, False)
+        for step in range(STEPS):
+            g, pair = divmod(step, 2)
+            last = step == STEPS - 1
+            new_laplacian(g, pair)
+            if not last:
+                for local in BOTH:
+                    form_diagonal(g, pair, local)
+                for local in BOTH:
+                    form_rest(g, pair, local)
+                add_eye(g, pair, BOTH)
+                spread_roots((step + 1) // 2, (step + 1) % 2)
+            if pair == OUTER and scalar_first(g) < FEATS:
+                regroup_on_scalar(g, slice(scalar_first(g), FEATS))
+            if g + 2 < GRAPHS:
+                for place in range(GROUP * pair, GROUP * pair + GROUP):
+                    if (g, place) != (0, 0):
+                        row_sum(g + 2, place)
+                    if (g, place) == (0, 2):
+                        row_sum(2, 0)
+            if last:
+                for local in BOTH:
+                    form_diagonal(g, pair, local)
+                    form_rest(g, pair, local)
+                    add_eye(g, pair, (local,))
+                    transpose_laplacian(g, pair, (local,))
+            else:
+                transpose_laplacian(g, pair, BOTH)
+            if pair == INNER and g + 2 < GRAPHS:
+                root(g + 2)
+            if pair == INNER and g + 1 < GRAPHS:
+                if step == 1:
+                    follow_first_pair(g, pair)
                 else:
-                    mx_pass(g, pair, 1)
-                    store(g, pair, 0, False)
-            if step + 1 < STEPS:
+                    follow_vector(g - 1, INNER)
+                new_x_grouped(g + 1)
+                regroup_on_gpsimd(g + 1, slice(0, GPSIMD_FIRST))
+            if pair == OUTER and g > 0:
+                follow_vector(g - 1, OUTER)
+                regroup_on_gpsimd(g, slice(GPSIMD_FIRST, scalar_first(g)))
+            if pair == INNER:
+                quantise_x(g)
+            if step > 0:
+                g, pair = divmod(step - 1, 2)
+                quantise_laplacian(g, pair, BOTH)
+                for local in BOTH:
+                    acc = psum_o.tile([P, FEATS], F32)
+                    mx_pass(g, pair, local, acc)
+                    if last and local == 1:
+                        break
+                    store(g, pair, local, False)
+                    if local == 0 and pair == OUTER and g + 2 < GRAPHS:
+                        negate(g + 2)
+            if not last:
                 g, pair = divmod(step + 1, 2)
                 for place in range(GROUP * pair, GROUP * pair + GROUP):
-                    if g + 2 < GRAPHS and kind_of(g + 2, place) == "P":
+                    if g + 2 < GRAPHS and summed_by(g + 2, place) == "B":
                         add_blocks(g + 2, place)
-            if step == STEPS:
-                g = GRAPHS - 1
-                quantise_laplacian(g, 1)
-                store(g, 0, 1, True)
-                mx_pass(g, 1, 0)
-                mx_pass(g, 1, 1)
-                store(g, 1, 0, False)
-                store(g, 1, 1, True)
+
+        g = GRAPHS - 1
+        for local in BOTH:
+            quantise_laplacian(g, INNER, (local,))
+        store(g, OUTER, 1, True)
+        acc_first = psum_c.tile([P, FEATS], F32, name="spare")
+        mx_pass(g, INNER, 0, acc_first)
+        acc_last = psum_r.tile([P, FEATS], F32, name="r_cols_outer")
+        mx_pass(g, INNER, 1, acc_last)
+        store(g, INNER, 0, False)
+        store(g, INNER, 1, True)

@@ -29,8 +29,10 @@ BOTH = (0, 1)
 ROW_TILE = ((0, 3), (1, 2))
 DIAGONAL_BLOCK = ((0, 3), (3, 0))
 PLACE_OF_BLOCK = (0, 2, 3, 1)
-RUN = 4
+RUN = 8
 GPSIMD_FIRST = 224
+
+ALL_FEATS = slice(0, FEATS)
 
 FLOPS = 2 * GRAPHS * NODES * NODES * FEATS
 
@@ -44,7 +46,7 @@ def tile_cheblayer_pa_kernel(tc, x, adj, out):
         per_graph = ctx.enter_context(tc.tile_pool(name="per_graph", bufs=3))
         per_unit = ctx.enter_context(tc.tile_pool(name="per_unit", bufs=4))
         per_pair = ctx.enter_context(tc.tile_pool(name="per_pair", bufs=3))
-        results = ctx.enter_context(tc.tile_pool(name="results", bufs=GRAPHS * ROW_TILES))
+        results = ctx.enter_context(tc.tile_pool(name="results", bufs=GRAPHS * ROW_TILES + GROUP))
         psum_r = ctx.enter_context(tc.psum_pool(name="psum_r", bufs=1))
         psum_t = ctx.enter_context(tc.psum_pool(name="psum_t", bufs=2))
         psum_o = ctx.enter_context(tc.psum_pool(name="psum_o", bufs=2))
@@ -63,7 +65,7 @@ def tile_cheblayer_pa_kernel(tc, x, adj, out):
             nc.tensor.transpose(out=eye_pair[:, local, :], in_=eye_f32[:], identity=eye_f32[:])
 
         adj_of, x_of, degree_of, r_pos_of, r_neg_of, r_cols_of = {}, {}, {}, {}, {}, {}
-        lap_codes_of, lap_scales_of, acc_of, scaled_of, block_sum_of = {}, {}, {}, {}, {}
+        lap_codes_of, lap_scales_of, scaled_of, block_sum_of = {}, {}, {}, {}
         x_grouped_of, x_codes_of, x_scales_of, lap_of, lap_grouped_of = {}, {}, {}, {}, {}
 
         def load_adj(g):
@@ -148,18 +150,24 @@ def tile_cheblayer_pa_kernel(tc, x, adj, out):
             nc.scalar.mul(out=r_neg[:], in_=r_pos_of[g][:], mul=-1.0)
             r_neg_of[g] = r_neg
 
+        def spread_of(g):
+            return r_pos_of[g] if g == 0 else r_neg_of[g]
+
+        def scalar_of(g):
+            return r_neg_of[g] if g == 0 else r_pos_of[g]
+
         def spread_roots(g, pair):
             if pair == OUTER:
                 r_cols_outer = psum_r.tile([P, NODES], F32, name="r_cols_outer")
                 r_cols = r_cols_outer
             else:
-                r_cols_inner = psum_r.tile([P, NODES], F32)
+                r_cols_inner = psum_r.tile([P, NODES], F32, name="r_cols_inner")
                 r_cols = r_cols_inner
             for b in range(ROW_TILES):
                 place = PLACE_OF_BLOCK[(b + 2 * pair) % ROW_TILES]
                 nc.tensor.transpose(
                     out=r_cols[:, b * P : (b + 1) * P],
-                    in_=r_pos_of[g][:, place : place + 1].to_broadcast([P, P]),
+                    in_=spread_of(g)[:, place : place + 1].to_broadcast([P, P]),
                     identity=eye_f32[:],
                 )
             r_cols_of[(g, pair)] = r_cols
@@ -217,7 +225,7 @@ def tile_cheblayer_pa_kernel(tc, x, adj, out):
             nc.vector.scalar_tensor_tensor(
                 out=dest,
                 in0=adj_of[g][:, place, cols],
-                scalar=r_neg_of[g][:, place : place + 1],
+                scalar=scalar_of(g)[:, place : place + 1],
                 in1=r_cols_of[(g, pair)][:, cols],
                 op0=ALU.mult,
                 op1=ALU.mult,
@@ -276,26 +284,25 @@ def tile_cheblayer_pa_kernel(tc, x, adj, out):
                 lap_codes_of[(g, pair, local)] = lap_codes[:, at : at + P]
                 lap_scales_of[(g, pair, local)] = lap_scales[:, at : at + P]
 
-        def mx_pass(g, pair, local, acc):
+        def mx_pass(g, pair, local, acc, cols=ALL_FEATS):
             nc.tensor.matmul_mx(
                 out=acc[:],
                 lhsT=lap_codes_of[(g, pair, local)].bitcast(FP8X4),
                 lhsT_scale=lap_scales_of[(g, pair, local)],
-                rhs=x_codes_of[g][:].bitcast(FP8X4),
-                rhs_scale=x_scales_of[g][:],
+                rhs=x_codes_of[g][:, cols].bitcast(FP8X4),
+                rhs_scale=x_scales_of[g][:, cols],
                 start=True,
                 stop=True,
             )
-            acc_of[(g, pair, local)] = acc
 
-        def store(g, pair, local, on_vector):
+        def store(g, pair, local, acc, on_vector, cols=ALL_FEATS):
             m = ROW_TILE[pair][local]
-            result = results.tile([P, FEATS], F32)
+            result = results.tile([P, cols.stop - cols.start], F32, name="result")
             if on_vector:
-                nc.vector.tensor_copy(out=result[:], in_=acc_of[(g, pair, local)][:])
+                nc.vector.tensor_copy(out=result[:], in_=acc[:])
             else:
-                nc.scalar.copy(out=result[:], in_=acc_of[(g, pair, local)][:])
-            nc.sync.dma_start(out=out[g, m * P : (m + 1) * P, :], in_=result[:])
+                nc.scalar.copy(out=result[:], in_=acc[:])
+            nc.sync.dma_start(out=out[g, m * P : (m + 1) * P, cols], in_=result[:])
 
         load_adj(0)
         load_adj(1)
@@ -360,27 +367,37 @@ def tile_cheblayer_pa_kernel(tc, x, adj, out):
             if step > 0:
                 g, pair = divmod(step - 1, 2)
                 quantise_laplacian(g, pair, BOTH)
+                if last:
+                    break
                 for local in BOTH:
-                    acc = psum_o.tile([P, FEATS], F32)
+                    acc = psum_o.tile([P, FEATS], F32, name="acc")
                     mx_pass(g, pair, local, acc)
-                    if last and local == 1:
-                        break
-                    store(g, pair, local, False)
+                    if step < STEPS - 2 or local == 0:
+                        store(g, pair, local, acc, False)
                     if local == 0 and pair == OUTER and g + 2 < GRAPHS:
                         negate(g + 2)
-            if not last:
-                g, pair = divmod(step + 1, 2)
-                for place in range(GROUP * pair, GROUP * pair + GROUP):
-                    if g + 2 < GRAPHS and summed_by(g + 2, place) == "B":
-                        add_blocks(g + 2, place)
+            g, pair = divmod(step + 1, 2)
+            for place in range(GROUP * pair, GROUP * pair + GROUP):
+                if g + 2 < GRAPHS and summed_by(g + 2, place) == "B":
+                    add_blocks(g + 2, place)
 
         g = GRAPHS - 1
+        store(g - 1, INNER, 1, acc, False)
+        acc_0 = psum_c.tile([P, FEATS], F32, name="spare")
+        acc_1 = psum_r.tile([P, FEATS], F32, name="r_cols_outer")
+        acc_2 = psum_o.tile([P, FEATS], F32, name="acc")
+        acc_left = psum_r.tile([P, FEATS // 2], F32, name="r_cols_inner")
+        acc_right = psum_t.tile([P, FEATS // 2], F32, name="lap_t")
+        left, right = slice(0, FEATS // 2), slice(FEATS // 2, FEATS)
         for local in BOTH:
             quantise_laplacian(g, INNER, (local,))
-        store(g, OUTER, 1, True)
-        acc_first = psum_c.tile([P, FEATS], F32, name="spare")
-        mx_pass(g, INNER, 0, acc_first)
-        acc_last = psum_r.tile([P, FEATS], F32, name="r_cols_outer")
-        mx_pass(g, INNER, 1, acc_last)
-        store(g, INNER, 0, False)
-        store(g, INNER, 1, True)
+        mx_pass(g, OUTER, 0, acc_0)
+        mx_pass(g, OUTER, 1, acc_1)
+        mx_pass(g, INNER, 0, acc_2)
+        mx_pass(g, INNER, 1, acc_left, left)
+        mx_pass(g, INNER, 1, acc_right, right)
+        store(g, OUTER, 0, acc_0, True)
+        store(g, OUTER, 1, acc_1, False)
+        store(g, INNER, 0, acc_2, True)
+        store(g, INNER, 1, acc_left, False, left)
+        store(g, INNER, 1, acc_right, True, right)

@@ -30,7 +30,7 @@ ROW_TILE = ((0, 3), (1, 2))
 DIAGONAL_BLOCK = ((0, 3), (3, 0))
 PLACE_OF_BLOCK = (0, 2, 3, 1)
 RUN = 8
-GPSIMD_FIRST = 224
+GPSIMD_FIRST = 208
 
 ALL_FEATS = slice(0, FEATS)
 
@@ -193,7 +193,7 @@ def tile_cheblayer_pa_kernel(tc, x, adj, out):
             )
 
         def scalar_first(g):
-            return FEATS - (0 if g + 2 < GRAPHS else 128)
+            return FEATS - (64 if g + 2 < GRAPHS else 128)
 
         def follow_vector(g, pair):
             seen = per_pair.tile([P, 1], U32)
@@ -334,7 +334,7 @@ def tile_cheblayer_pa_kernel(tc, x, adj, out):
                     form_rest(g, pair, local)
                 add_eye(g, pair, BOTH)
                 spread_roots((step + 1) // 2, (step + 1) % 2)
-            if pair == OUTER and scalar_first(g) < FEATS:
+            if pair == OUTER and g > 0:
                 regroup_on_scalar(g, slice(scalar_first(g), FEATS))
             if g + 2 < GRAPHS:
                 for place in range(GROUP * pair, GROUP * pair + GROUP):

from contextlib import ExitStack

import concourse.mybir as mybir
from concourse.masks import make_identity

F32 = mybir.dt.float32
BF16 = mybir.dt.bfloat16
U32 = mybir.dt.uint32
U8 = mybir.dt.uint8
FP8X4 = mybir.dt.float8_e4m3fn_x4
ALU = mybir.AluOpType
ACT = mybir.ActivationFunctionType

P = 128
GRAPHS = 8
NODES = 512
FEATS = 512
ROW_TILES = NODES // P
PACK = 4
HALVES = 2
HALF = NODES // HALVES
PAIR = 2
OWN_BLOCK = 8
EPS = 1e-6
GROUP = 2
OUTER, INNER = 0, 1
STEPS = 2 * GRAPHS
BOTH = (0, 1)
ROW_TILE = ((0, 3), (1, 2))
DIAGONAL_BLOCK = ((0, 3), (3, 0))
PLACE_OF_BLOCK = (0, 2, 3, 1)
RUN = 8
GPSIMD_FIRST = 208

ALL_FEATS = slice(0, FEATS)

FLOPS = 2 * GRAPHS * NODES * NODES * FEATS


def tile_cheblayer_pa_kernel(tc, x, adj, out):
    nc = tc.nc
    with ExitStack() as ctx:
        ctx.enter_context(tc.manual_schedule())
        const = ctx.enter_context(tc.tile_pool(name="const", bufs=1))
        loads = ctx.enter_context(tc.tile_pool(name="loads", bufs=GRAPHS))
        per_graph = ctx.enter_context(tc.tile_pool(name="per_graph", bufs=3))
        per_unit = ctx.enter_context(tc.tile_pool(name="per_unit", bufs=4))
        per_pair = ctx.enter_context(tc.tile_pool(name="per_pair", bufs=3))
        results = ctx.enter_context(tc.tile_pool(name="results", bufs=GRAPHS * ROW_TILES + GROUP))
        psum_r = ctx.enter_context(tc.psum_pool(name="psum_r", bufs=1))
        psum_t = ctx.enter_context(tc.psum_pool(name="psum_t", bufs=2))
        psum_o = ctx.enter_context(tc.psum_pool(name="psum_o", bufs=2))
        psum_c = ctx.enter_context(tc.psum_pool(name="psum_c", bufs=1))

        eye_f32 = const.tile([P, P], F32)
        make_identity(nc, eye_f32[:])
        eps = const.tile([P, 1], F32)
        nc.vector.memset(eps[:], EPS)
        table_warmer = const.tile([P, 1], F32)
        nc.scalar.activation(out=table_warmer[:], in_=eps[:], func=ACT.Abs_reciprocal_sqrt)
        eye_bf16 = const.tile([P, P], BF16)
        nc.scalar.copy(out=eye_bf16[:], in_=eye_f32[:])
        eye_pair = psum_c.tile([P, GROUP, P], F32)
        for local in BOTH:
            nc.tensor.transpose(out=eye_pair[:, local, :], in_=eye_f32[:], identity=eye_f32[:])

        adj_of, x_of, degree_of, r_pos_of, r_neg_of, r_cols_of = {}, {}, {}, {}, {}, {}
        lap_codes_of, lap_scales_of, scaled_of, block_sum_of = {}, {}, {}, {}
        x_grouped_of, x_codes_of, x_scales_of, lap_of, lap_grouped_of = {}, {}, {}, {}, {}

        def load_adj(g):
            adj_sb = loads.tile([P, ROW_TILES, NODES], BF16)
            rows = adj[g].rearrange("(m p) j -> p m j", p=P)
            if g == 0:
                for local in BOTH:
                    nc.sync.dma_start(out=adj_sb[:, local, :], in_=rows[:, ROW_TILE[OUTER][local], :])
            else:
                nc.sync.dma_start(out=adj_sb[:, 0:GROUP, :], in_=rows[:, 0:ROW_TILES:3, :])
            for half in range(HALVES):
                nc.sync.dma_start(
                    out=adj_sb[:, GROUP:ROW_TILES, half * HALF : (half + 1) * HALF],
                    in_=rows[:, 1:3, (1 - half) * HALF : (2 - half) * HALF],
                )
            adj_of[g] = adj_sb

        def load_x(g):
            x_sb = loads.tile([P, PACK, FEATS], BF16)
            nc.sync.dma_start(
                out=x_sb[:].rearrange("p (u e) f -> p u e f", u=HALVES),
                in_=x[g].rearrange("(u p e) f -> p u e f", u=HALVES, e=PAIR),
            )
            x_of[g] = x_sb

        def summed_by(g, place):
            if g == 0:
                return "VVVS"[place]
            if g == 1 or (g == 2 and place < GROUP):
                return "VSVS"[place]
            return "VBSB"[place]

        def add_blocks(g, place):
            block_sum = psum_c.tile([P, P], F32, name="spare")
            for b in range(ROW_TILES):
                nc.tensor.matmul(
                    out=block_sum[:],
                    lhsT=eye_bf16[:],
                    rhs=adj_of[g][:, place, b * P : (b + 1) * P],
                    start=b == 0,
                    stop=b == ROW_TILES - 1,
                )
            block_sum_of[(g, place)] = block_sum

        def row_sum(g, place):
            if g not in degree_of:
                degree = per_graph.tile([P, ROW_TILES, OWN_BLOCK], F32)
                degree_of[g] = degree
            total = degree_of[g][:, place, 0:1]
            engine = summed_by(g, place)
            if engine == "V":
                unread_v = per_unit.tile([P, NODES], BF16)
                nc.vector.tensor_scalar(
                    out=unread_v[:],
                    in0=adj_of[g][:, place, :],
                    scalar1=1.0,
                    scalar2=None,
                    op0=ALU.mult,
                    op1=ALU.add,
                    accum_out=total,
                )
            elif engine == "S":
                unread_s = per_unit.tile([P, NODES], BF16)
                nc.scalar.activation(out=unread_s[:], in_=adj_of[g][:, place, :], func=ACT.Copy, accum_out=total)
            else:
                unread_b = per_unit.tile([P, P], F32)
                nc.scalar.activation(out=unread_b[:], in_=block_sum_of[(g, place)][:], func=ACT.Copy, accum_out=total)

        def root(g):
            r_pos = per_graph.tile([P, ROW_TILES], F32)
            nc.scalar.activation(
                out=r_pos[:],
                in_=degree_of[g][:, :, 0],
                func=ACT.Abs_reciprocal_sqrt,
                bias=eps[:, 0:1],
                scale=1.0,
            )
            r_pos_of[g] = r_pos

        def negate(g):
            r_neg = per_graph.tile([P, ROW_TILES], F32)
            nc.scalar.mul(out=r_neg[:], in_=r_pos_of[g][:], mul=-1.0)
            r_neg_of[g] = r_neg

        def spread_of(g):
            return r_pos_of[g] if g == 0 else r_neg_of[g]

        def scalar_of(g):
            return r_neg_of[g] if g == 0 else r_pos_of[g]

        def spread_roots(g, pair):
            if pair == OUTER:
                r_cols_outer = psum_r.tile([P, NODES], F32, name="r_cols_outer")
                r_cols = r_cols_outer
            else:
                r_cols_inner = psum_r.tile([P, NODES], F32, name="r_cols_inner")
                r_cols = r_cols_inner
            for b in range(ROW_TILES):
                place = PLACE_OF_BLOCK[(b + 2 * pair) % ROW_TILES]
                nc.tensor.transpose(
                    out=r_cols[:, b * P : (b + 1) * P],
                    in_=spread_of(g)[:, place : place + 1].to_broadcast([P, P]),
                    identity=eye_f32[:],
                )
            r_cols_of[(g, pair)] = r_cols

        def new_x_grouped(g):
            x_grouped = per_graph.tile([P, FEATS, PACK], BF16, align_bytes=64)
            x_grouped_of[g] = x_grouped

        def regroup_on_gpsimd(g, cols):
            nc.gpsimd.tensor_scalar(
                out=x_grouped_of[g][:, cols, :].rearrange("p (c i) t -> p c t i", i=RUN),
                in0=x_of[g][:, :, cols].rearrange("p t (c i) -> p c t i", i=RUN),
                scalar1=1.0,
                scalar2=0.0,
                op0=ALU.mult,
                op1=ALU.add,
            )

        def regroup_on_scalar(g, cols):
            nc.scalar.copy(
                out=x_grouped_of[g][:, cols, :].rearrange("p (c i) t -> p c t i", i=RUN),
                in_=x_of[g][:, :, cols].rearrange("p t (c i) -> p c t i", i=RUN),
            )

        def scalar_first(g):
            return FEATS - (64 if g + 2 < GRAPHS else 128)

        def follow_vector(g, pair):
            seen = per_pair.tile([P, 1], U32)
            nc.gpsimd.tensor_copy(out=seen[:], in_=lap_codes_of[(g, pair, 0)][:, 0:1])

        def follow_first_pair(g, pair):
            seen_first = per_pair.tile([P, 1], F32)
            nc.gpsimd.tensor_copy(out=seen_first[:], in_=scaled_of[(g, pair)][:, 0, 0:1])

        def quantise_x(g):
            x_codes = per_graph.tile([P, FEATS], U32, align_bytes=64)
            x_scales = per_graph.tile([P, FEATS], U8, align_bytes=64)
            nc.vector.quantize_mx(
                out=x_codes[:].bitcast(FP8X4),
                scales=x_scales[:],
                in_=x_grouped_of[g][:].rearrange("p f t -> p (f t)"),
            )
            x_codes_of[g] = x_codes
            x_scales_of[g] = x_scales

        def new_laplacian(g, pair):
            lap_pair = per_pair.tile([P, GROUP * ROW_TILES, P], BF16)
            scaled = per_pair.tile([P, GROUP, P], F32)
            lap_of[(g, pair)] = lap_pair
            scaled_of[(g, pair)] = scaled

        def scale_columns(g, pair, local, cols, dest):
            place = GROUP * pair + local
            nc.vector.scalar_tensor_tensor(
                out=dest,
                in0=adj_of[g][:, place, cols],
                scalar=scalar_of(g)[:, place : place + 1],
                in1=r_cols_of[(g, pair)][:, cols],
                op0=ALU.mult,
                op1=ALU.mult,
            )

        def form_diagonal(g, pair, local):
            b = DIAGONAL_BLOCK[pair][local]
            scale_columns(g, pair, local, slice(b * P, (b + 1) * P), scaled_of[(g, pair)][:, local, :])

        def form_rest(g, pair, local):
            first = 1 if DIAGONAL_BLOCK[pair][local] == 0 else 0
            blocks = lap_of[(g, pair)][:, local * ROW_TILES + first : local * ROW_TILES + first + ROW_TILES - 1, :]
            cols = slice(first * P, (first + ROW_TILES - 1) * P)
            scale_columns(g, pair, local, cols, blocks.rearrange("p b c -> p (b c)"))

        def add_eye(g, pair, tiles):
            first = tiles[0] * ROW_TILES + DIAGONAL_BLOCK[pair][tiles[0]]
            last = tiles[-1] * ROW_TILES + DIAGONAL_BLOCK[pair][tiles[-1]]
            nc.vector.tensor_tensor(
                out=lap_of[(g, pair)][:, first : last + 1 : max(last - first, 1), :],
                in0=scaled_of[(g, pair)][:, tiles[0] : tiles[-1] + 1, :],
                in1=eye_pair[:, tiles[0] : tiles[-1] + 1, :],
                op=ALU.add,
            )

        def transpose_laplacian(g, pair, tiles):
            rows = lap_of[(g, pair)][:].rearrange("p b c -> p (b c)").bitcast(F32)
            words = NODES // PAIR
            width = len(tiles) * P
            lap_t = psum_t.tile([P, HALVES, width], F32, name="lap_t")
            for local in tiles:
                at = (local - tiles[0]) * P
                for u in range(HALVES):
                    start = local * words + (u + pair) % HALVES * P
                    nc.tensor.transpose(
                        out=lap_t[:, u, at : at + P], in_=rows[:, start : start + P], identity=eye_f32[:]
                    )
            lap_grouped = per_pair.tile([P, width * PACK], BF16, align_bytes=64, name="lap_grouped")
            nc.scalar.copy(
                out=lap_grouped[:].bitcast(F32).rearrange("p (c u) -> p c u", u=HALVES),
                in_=lap_t[:].rearrange("p u c -> p c u"),
            )
            lap_grouped_of[(g, pair, tiles[0])] = lap_grouped

        def quantise_laplacian(g, pair, tiles):
            width = len(tiles) * P
            lap_codes = per_pair.tile([P, width], U32, align_bytes=64, name="lap_codes")
            lap_scales = per_pair.tile([P, width], U8, align_bytes=64, name="lap_scales")
            nc.vector.quantize_mx(
                out=lap_codes[:].bitcast(FP8X4),
                scales=lap_scales[:],
                in_=lap_grouped_of[(g, pair, tiles[0])][:],
            )
            for local in tiles:
                at = (local - tiles[0]) * P
                lap_codes_of[(g, pair, local)] = lap_codes[:, at : at + P]
                lap_scales_of[(g, pair, local)] = lap_scales[:, at : at + P]

        def mx_pass(g, pair, local, acc, cols=ALL_FEATS):
            nc.tensor.matmul_mx(
                out=acc[:],
                lhsT=lap_codes_of[(g, pair, local)].bitcast(FP8X4),
                lhsT_scale=lap_scales_of[(g, pair, local)],
                rhs=x_codes_of[g][:, cols].bitcast(FP8X4),
                rhs_scale=x_scales_of[g][:, cols],
                start=True,
                stop=True,
            )

        def store(g, pair, local, acc, on_vector, cols=ALL_FEATS):
            m = ROW_TILE[pair][local]
            result = results.tile([P, cols.stop - cols.start], F32, name="result")
            if on_vector:
                nc.vector.tensor_copy(out=result[:], in_=acc[:])
            else:
                nc.scalar.copy(out=result[:], in_=acc[:])
            nc.sync.dma_start(out=out[g, m * P : (m + 1) * P, cols], in_=result[:])

        load_adj(0)
        load_adj(1)
        load_x(0)
        for g in range(1, GRAPHS):
            load_x(g)
            if g + 1 < GRAPHS:
                load_adj(g + 1)

        for g in range(2):
            for place in range(ROW_TILES):
                row_sum(g, place)
            root(g)
            negate(g)
            if g == 0:
                spread_roots(0, OUTER)
        new_x_grouped(0)
        regroup_on_gpsimd(0, slice(0, FEATS // 2))
        regroup_on_scalar(0, slice(FEATS // 2, FEATS))

        for step in range(STEPS):
            g, pair = divmod(step, 2)
            last = step == STEPS - 1
            new_laplacian(g, pair)
            if not last:
                for local in BOTH:
                    form_diagonal(g, pair, local)
                for local in BOTH:
                    form_rest(g, pair, local)
                add_eye(g, pair, BOTH)
                spread_roots((step + 1) // 2, (step + 1) % 2)
            if pair == OUTER and g > 0:
                regroup_on_scalar(g, slice(scalar_first(g), FEATS))
            if g + 2 < GRAPHS:
                for place in range(GROUP * pair, GROUP * pair + GROUP):
                    if (g, place) != (0, 0):
                        row_sum(g + 2, place)
                    if (g, place) == (0, 2):
                        row_sum(2, 0)
            if last:
                for local in BOTH:
                    form_diagonal(g, pair, local)
                    form_rest(g, pair, local)
                    add_eye(g, pair, (local,))
                    transpose_laplacian(g, pair, (local,))
            else:
                transpose_laplacian(g, pair, BOTH)
            if pair == INNER and g + 2 < GRAPHS:
                root(g + 2)
            if pair == INNER and g + 1 < GRAPHS:
                if step == 1:
                    follow_first_pair(g, pair)
                else:
                    follow_vector(g - 1, INNER)
                new_x_grouped(g + 1)
                regroup_on_gpsimd(g + 1, slice(0, GPSIMD_FIRST))
            if pair == OUTER and g > 0:
                follow_vector(g - 1, OUTER)
                regroup_on_gpsimd(g, slice(GPSIMD_FIRST, scalar_first(g)))
            if pair == INNER:
                quantise_x(g)
            if step > 0:
                g, pair = divmod(step - 1, 2)
                quantise_laplacian(g, pair, BOTH)
                if last:
                    break
                for local in BOTH:
                    acc = psum_o.tile([P, FEATS], F32, name="acc")
                    mx_pass(g, pair, local, acc)
                    if step < STEPS - 2 or local == 0:
                        store(g, pair, local, acc, False)
                    if local == 0 and pair == OUTER and g + 2 < GRAPHS:
                        negate(g + 2)
            g, pair = divmod(step + 1, 2)
            for place in range(GROUP * pair, GROUP * pair + GROUP):
                if g + 2 < GRAPHS and summed_by(g + 2, place) == "B":
                    add_blocks(g + 2, place)

        g = GRAPHS - 1
        store(g - 1, INNER, 1, acc, False)
        acc_0 = psum_c.tile([P, FEATS], F32, name="spare")
        acc_1 = psum_r.tile([P, FEATS], F32, name="r_cols_outer")
        acc_2 = psum_o.tile([P, FEATS], F32, name="acc")
        acc_left = psum_r.tile([P, FEATS // 2], F32, name="r_cols_inner")
        acc_right = psum_t.tile([P, FEATS // 2], F32, name="lap_t")
        left, right = slice(0, FEATS // 2), slice(FEATS // 2, FEATS)
        for local in BOTH:
            quantise_laplacian(g, INNER, (local,))
        mx_pass(g, OUTER, 0, acc_0)
        mx_pass(g, OUTER, 1, acc_1)
        mx_pass(g, INNER, 0, acc_2)
        mx_pass(g, INNER, 1, acc_left, left)
        mx_pass(g, INNER, 1, acc_right, right)
        store(g, OUTER, 0, acc_0, True)
        store(g, OUTER, 1, acc_1, False)
        store(g, INNER, 0, acc_2, True)
        store(g, INNER, 1, acc_left, False, left)
        store(g, INNER, 1, acc_right, True, right)
